import numpy as np
import ml_dtypes


def mxq(x, axis, fmt="e4m3"):
    dtype, down = {"e4m3": (ml_dtypes.float8_e4m3fn, 7), "e5m2": (ml_dtypes.float8_e5m2, 14)}[fmt]
    v = np.moveaxis(np.asarray(x, np.float32).astype(ml_dtypes.bfloat16).astype(np.float64), axis, -1)
    blocks = v.reshape(v.shape[:-1] + (-1, 32))
    amax = np.abs(blocks).max(-1, keepdims=True)
    byte = np.maximum(np.where(amax > 0, np.frexp(amax)[1] - 1 + 127, 0) - down, 1)
    scale = np.exp2(byte - 127.0)
    codes = (blocks / scale).astype(np.float32).astype(dtype).astype(np.float64)
    return np.moveaxis((codes * scale).reshape(v.shape), -1, axis)


WIDE = False


def mx_kscale(k):
    if not WIDE:
        return np.ones(k)
    levels = np.array([10, -10, 5, -5, 0])
    a = np.random.permutation(np.resize(levels, k // 512 * 4)).reshape(k // 512, 4)
    idx = np.arange(k)
    return np.exp2(a[idx // 512, idx % 128 // 32])


BF16 = ml_dtypes.bfloat16


def bf(x):
    return np.asarray(x, np.float32).astype(BF16)


def f64(x):
    return np.asarray(x).astype(np.float64)


N, M, P = 512, 8, 512
EPS = 1e-6


def setup_inputs():
    s = mx_kscale(P)
    a = np.log2(s) / 10.0
    u, v = np.maximum(a, 0.0), np.maximum(-a, 0.0)
    x = np.random.standard_normal((N * M, P)).reshape(N, M, P)
    x[0::2] = (x[0::2] + u) * s
    x[1::2] = (x[1::2] + v) / s
    nrm = np.sqrt(N / 2.0 * np.sum(s ** 2.0 * (1.0 / M + u * u) + s ** -2.0 * (1.0 / M + v * v)))
    q = 0.5 * (np.sum(u * u) + np.sum(v * v))
    sd = np.sqrt((P + q) / M + q) / nrm
    return {"inputs": bf(x.reshape(N * M, P)),
            "w": bf(-(0.2 + 0.1 * np.random.random(1)) / sd),
            "b": bf(0.5 + 0.1 * np.random.standard_normal(1))}


def reference(inputs, w, b):
    e = f64(inputs).reshape(N, M, P)
    cmean = np.mean(e, axis=1)
    norm = np.sqrt(np.maximum(np.sum(cmean * cmean), EPS))
    centroids = cmean / norm
    S = (mxq(e, 2, "e4m3") @ mxq(centroids, 1, "e4m3").T).reshape(N * M, N)
    return np.clip(np.abs(f64(w)) * S + f64(b), 0.0, 1.0)

@@ -1,0 +1,178 @@
+from contextlib import ExitStack
+
+import concourse.mybir as mybir
+from concourse.masks import make_identity
+
+F32 = mybir.dt.float32
+BF16 = mybir.dt.bfloat16
+U32 = mybir.dt.uint32
+U8 = mybir.dt.uint8
+FP8X4 = mybir.dt.float8_e4m3fn_x4
+ALU = mybir.AluOpType
+ACT = mybir.ActivationFunctionType
+AX = mybir.AxisListType
+
+P = 128
+ROWS = 4096
+K = 512
+SPK = 512
+EPS = 1e-6
+CH_ROWS = 256
+NCH = ROWS // CH_ROWS
+FLOPS = 2 * ROWS * K * SPK
+
+
+def tile_similaritymatrixlayer_kernel(tc, inputs, w, b, out):
+    nc = tc.nc
+    with ExitStack() as ctx:
+        const = ctx.enter_context(tc.tile_pool(name="const", bufs=1))
+        data = ctx.enter_context(tc.tile_pool(name="data", bufs=1))
+        psum = ctx.enter_context(tc.psum_pool(name="psum", bufs=4))
+
+        x = []
+        for c in range(NCH):
+            xc = data.tile([P, 2 * K], BF16, name="x%d" % c)
+            nc.sync.dma_start(
+                out=xc[:],
+                in_=inputs[CH_ROWS * c : CH_ROWS * (c + 1), :].rearrange("(p j) k -> p (j k)", j=2),
+            )
+            x.append(xc)
+        w16 = const.tile([P, 1], BF16, name="w16")
+        b16 = const.tile([P, 1], BF16, name="b16")
+        nc.scalar.dma_start(out=w16[:], in_=w.partition_broadcast(P))
+        nc.scalar.dma_start(out=b16[:], in_=b.partition_broadcast(P))
+
+        warm = const.tile([P, 1], F32, name="warm")
+        nc.vector.memset(warm[:], 1.0)
+        nc.scalar.activation(out=warm[:], in_=warm[:], func=ACT.Sqrt)
+        ident = const.tile([P, P], F32, name="ident")
+        make_identity(nc, ident[:])
+        avg_f = const.tile([P, 32], F32, name="avg_f")
+        nc.vector.tensor_reduce(
+            out=avg_f[:], in_=ident[:].rearrange("p (s i) -> p s i", i=4), axis=AX.X, op=ALU.add
+        )
+        avg = const.tile([P, 32], BF16, name="avg")
+        nc.vector.tensor_scalar(out=avg[:], in0=avg_f[:], scalar1=0.125, scalar2=None, op0=ALU.mult)
+        ones = const.tile([P, P], F32, name="ones")
+        nc.vector.memset(ones[:], 1.0)
+
+        wf = const.tile([P, 1], F32, name="wf")
+        nc.vector.tensor_copy(out=wf[:], in_=w16[:])
+        negw = const.tile([P, 1], F32, name="negw")
+        nc.vector.tensor_scalar(out=negw[:], in0=wf[:], scalar1=-1.0, scalar2=None, op0=ALU.mult)
+        absw = const.tile([P, 1], F32, name="absw")
+        nc.vector.tensor_tensor(out=absw[:], in0=wf[:], in1=negw[:], op=ALU.max)
+        bias = const.tile([P, 1], F32, name="bias")
+        nc.vector.tensor_copy(out=bias[:], in_=b16[:])
+
+        cm = []
+        for bk in range(4):
+            cmb = psum.tile([P, 4, 4, 32], F32, tag="cm", name="cm%d" % bk)
+            cm.append(cmb)
+        ss = const.tile([P, NCH], F32, name="ss")
+        junk = const.tile([P, 4, 32], F32, name="junk")
+        for c in range(NCH):
+            bk, g = c % 4, c // 4
+            xv = x[c][:].rearrange("p (j u q e) -> p j u e q", j=2, u=2, q=P, e=2)
+            for u in range(2):
+                for e in range(2):
+                    for j in range(2):
+                        nc.tensor.matmul(
+                            out=cm[bk][:, 2 * u + e, g, :],
+                            lhsT=xv[:, j, u, e, :],
+                            rhs=avg[:],
+                            start=(j == 0),
+                            stop=(j == 1),
+                        )
+            nc.scalar.activation(
+                out=junk[:], in_=cm[bk][:, :, g, :], func=ACT.Square, accum_out=ss[:, c : c + 1]
+            )
+
+        tot_ps = psum.tile([P, NCH], F32, tag="xt", name="tot_ps")
+        nc.tensor.matmul(out=tot_ps[:], lhsT=ones[:], rhs=ss[:], start=True, stop=True)
+        tot = const.tile([P, 1], F32, name="tot")
+        nc.vector.tensor_reduce(out=tot[:], in_=tot_ps[:], axis=AX.X, op=ALU.add)
+        nc.vector.tensor_scalar(out=tot[:], in0=tot[:], scalar1=EPS, scalar2=None, op0=ALU.max)
+        norm = const.tile([P, 1], F32, name="norm")
+        nc.scalar.activation(out=norm[:], in_=tot[:], func=ACT.Sqrt)
+        rnorm = const.tile([P, 1], F32, name="rnorm")
+        nc.vector.reciprocal(out=rnorm[:], in_=norm[:])
+
+        cent = data.tile([P, SPK * 4], BF16, name="cent", align_bytes=64)
+        cq = data.tile([P, SPK], U32, name="cq", align_bytes=64)
+        cs = data.tile([P, SPK], U8, name="cs", align_bytes=64)
+        centv = cent[:].rearrange("q (g k i t) -> q k g i t", g=4, k=4, i=32, t=4)
+        for bk in range(4):
+            src = cm[bk][:].rearrange("q t g i -> q g i t")
+            if bk % 2 == 0:
+                nc.vector.tensor_scalar(
+                    out=centv[:, bk], in0=src, scalar1=rnorm[:, 0:1], scalar2=None, op0=ALU.mult
+                )
+            else:
+                nc.scalar.activation(out=centv[:, bk], in_=src, func=ACT.Copy, scale=rnorm[:, 0:1])
+        nc.vector.quantize_mx(out=cq[:].bitcast(FP8X4), scales=cs[:], in_=cent[:])
+
+        xq = []
+        xs = []
+        grp = []
+
+        def quantise(c):
+            nc.vector.quantize_mx(out=xq[c][:].bitcast(FP8X4), scales=xs[c][:], in_=grp[c][:])
+
+        for c in range(NCH):
+            xw = x[c][:].bitcast(F32)
+            xt = psum.tile([P, 2, 2, P], F32, tag="xt", name="xt")
+            for j in range(2):
+                for u in range(2):
+                    nc.tensor.transpose(
+                        xt[:, j, u, :], xw[:, 256 * j + P * u : 256 * j + P * (u + 1)], ident[:]
+                    )
+            gc = data.tile([P, 2 * P * 4], BF16, name="g%d" % c, align_bytes=64)
+            grp.append(gc)
+            xqc = data.tile([P, 2 * P], U32, name="xq%d" % c, align_bytes=64)
+            xq.append(xqc)
+            xsc = data.tile([P, 2 * P], U8, name="xs%d" % c, align_bytes=64)
+            xs.append(xsc)
+            dst = gc[:].bitcast(F32).rearrange("q (j r u) -> q j r u", j=2, r=P, u=2)
+            srcx = xt[:].rearrange("q j u r -> q j r u")
+            if c % 8 in (1, 4, 6):
+                nc.vector.tensor_copy(out=dst, in_=srcx)
+            else:
+                nc.scalar.copy(out=dst, in_=srcx)
+            if c > 0:
+                quantise(c - 1)
+        quantise(NCH - 1)
+
+        for c in range(NCH):
+            oc = data.tile([P, 2, SPK], F32, name="o%d" % c)
+            for j in range(2):
+                acc = psum.tile([P, SPK], F32, tag="cm", name="acc")
+                nc.tensor.matmul_mx(
+                    out=acc[:],
+                    lhsT=xq[c][:, P * j : P * (j + 1)].bitcast(FP8X4),
+                    lhsT_scale=xs[c][:, P * j : P * (j + 1)],
+                    rhs=cq[:].bitcast(FP8X4),
+                    rhs_scale=cs[:],
+                    start=True,
+                    stop=True,
+                )
+                if (2 * c + j) % 4 == 3:
+                    nc.vector.tensor_scalar(
+                        out=oc[:, j, :],
+                        in0=acc[:],
+                        scalar1=absw[:, 0:1],
+                        scalar2=bias[:, 0:1],
+                        op0=ALU.mult,
+                        op1=ALU.add,
+                    )
+                else:
+                    nc.scalar.activation(
+                        out=oc[:, j, :], in_=acc[:], func=ACT.Relu, scale=absw[:, 0:1], bias=bias[:, 0:1]
+                    )
+            nc.vector.tensor_scalar(
+                out=oc[:], in0=oc[:], scalar1=0.0, scalar2=1.0, op0=ALU.max, op1=ALU.min
+            )
+            nc.sync.dma_start(
+                out=out[CH_ROWS * c : CH_ROWS * (c + 1), :].rearrange("(p j) n -> p j n", j=2),
+                in_=oc[:],
+            )

@@ -17,8 +17,8 @@ ROWS = 4096
 K = 512
 SPK = 512
 EPS = 1e-6
-CH_ROWS = 256
-NCH = ROWS // CH_ROWS
+NU = 8
+NCH = 16
 FLOPS = 2 * ROWS * K * SPK
 
 
@@ -28,15 +28,21 @@ def tile_similaritymatrixlayer_kernel(tc, inputs, w, b, out):
         const = ctx.enter_context(tc.tile_pool(name="const", bufs=1))
         data = ctx.enter_context(tc.tile_pool(name="data", bufs=1))
         psum = ctx.enter_context(tc.psum_pool(name="psum", bufs=4))
+        ctx.enter_context(tc.manual_schedule())
 
         x = []
-        for c in range(NCH):
-            xc = data.tile([P, 2 * K], BF16, name="x%d" % c)
-            nc.sync.dma_start(
-                out=xc[:],
-                in_=inputs[CH_ROWS * c : CH_ROWS * (c + 1), :].rearrange("(p j) k -> p (j k)", j=2),
-            )
-            x.append(xc)
+        for u in range(NU):
+            xu = data.tile([P, 4 * K], BF16, name="x%d" % u)
+            x.append(xu)
+            rows = inputs[512 * u : 512 * (u + 1), :]
+            if u % 2 == 0:
+                nc.sync.dma_start(out=xu[:], in_=rows.rearrange("(p a) k -> p (a k)", a=4))
+            else:
+                for h in range(2):
+                    nc.sync.dma_start(
+                        out=xu[:, 2 * K * h : 2 * K * (h + 1)],
+                        in_=rows[256 * h : 256 * (h + 1), :].rearrange("(p j) k -> p (j k)", j=2),
+                    )
         w16 = const.tile([P, 1], BF16, name="w16")
         b16 = const.tile([P, 1], BF16, name="b16")
         nc.scalar.dma_start(out=w16[:], in_=w.partition_broadcast(P))
@@ -47,132 +53,212 @@ def tile_similaritymatrixlayer_kernel(tc, inputs, w, b, out):
         nc.scalar.activation(out=warm[:], in_=warm[:], func=ACT.Sqrt)
         ident = const.tile([P, P], F32, name="ident")
         make_identity(nc, ident[:])
-        avg_f = const.tile([P, 32], F32, name="avg_f")
-        nc.vector.tensor_reduce(
-            out=avg_f[:], in_=ident[:].rearrange("p (s i) -> p s i", i=4), axis=AX.X, op=ALU.add
-        )
-        avg = const.tile([P, 32], BF16, name="avg")
-        nc.vector.tensor_scalar(out=avg[:], in0=avg_f[:], scalar1=0.125, scalar2=None, op0=ALU.mult)
+        avg = {}
+        for wd in (64, 32):
+            avg_f = const.tile([P, wd], F32, name="avg_f%d" % wd)
+            nc.vector.tensor_reduce(
+                out=avg_f[:], in_=ident[:].rearrange("p (s i) -> p s i", s=wd), axis=AX.X, op=ALU.add
+            )
+            avg_b = const.tile([P, wd], BF16, name="avg_b%d" % wd)
+            nc.vector.tensor_scalar(out=avg_b[:], in0=avg_f[:], scalar1=0.125, scalar2=None, op0=ALU.mult)
+            avg[wd] = avg_b
         ones = const.tile([P, P], F32, name="ones")
         nc.vector.memset(ones[:], 1.0)
 
         wf = const.tile([P, 1], F32, name="wf")
-        nc.vector.tensor_copy(out=wf[:], in_=w16[:])
         negw = const.tile([P, 1], F32, name="negw")
-        nc.vector.tensor_scalar(out=negw[:], in0=wf[:], scalar1=-1.0, scalar2=None, op0=ALU.mult)
         absw = const.tile([P, 1], F32, name="absw")
-        nc.vector.tensor_tensor(out=absw[:], in0=wf[:], in1=negw[:], op=ALU.max)
         bias = const.tile([P, 1], F32, name="bias")
-        nc.vector.tensor_copy(out=bias[:], in_=b16[:])
+
+        def scale_and_bias():
+            nc.vector.tensor_copy(out=wf[:], in_=w16[:])
+            nc.vector.tensor_scalar(out=negw[:], in0=wf[:], scalar1=-1.0, scalar2=None, op0=ALU.mult)
+            nc.vector.tensor_tensor(out=absw[:], in0=wf[:], in1=negw[:], op=ALU.max)
+            nc.vector.tensor_copy(out=bias[:], in_=b16[:])
 
         cm = []
         for bk in range(4):
-            cmb = psum.tile([P, 4, 4, 32], F32, tag="cm", name="cm%d" % bk)
+            cmb = psum.tile([P, 4, P], F32, tag="cm", name="cm%d" % bk)
             cm.append(cmb)
-        ss = const.tile([P, NCH], F32, name="ss")
-        junk = const.tile([P, 4, 32], F32, name="junk")
-        for c in range(NCH):
-            bk, g = c % 4, c // 4
-            xv = x[c][:].rearrange("p (j u q e) -> p j u e q", j=2, u=2, q=P, e=2)
-            for u in range(2):
-                for e in range(2):
-                    for j in range(2):
-                        nc.tensor.matmul(
-                            out=cm[bk][:, 2 * u + e, g, :],
-                            lhsT=xv[:, j, u, e, :],
-                            rhs=avg[:],
-                            start=(j == 0),
-                            stop=(j == 1),
-                        )
+        NSS = 12
+        ss = const.tile([P, NSS], F32, name="ss")
+        junk = const.tile([P, 4, 64], F32, name="junk")
+        ss_col = [0]
+
+        def means(u, h):
+            xv = x[u][:].rearrange("p (a u q e) -> p a u e q", a=4, u=2, q=P, e=2)
+            if u % 2 == 0:
+                bank, c0, wd, tiles = (0 if u % 4 == 0 else 3), 64 * (u // 4), 64, (0, 1, 2, 3)
+            else:
+                bank, c0, wd, tiles = 1 + h, 32 * (u // 2), 32, (2 * h, 2 * h + 1)
+            for t in range(4):
+                for n, a in enumerate(tiles):
+                    nc.tensor.matmul(
+                        out=cm[bank][:, t, c0 : c0 + wd],
+                        lhsT=xv[:, a, t // 2, t % 2, :],
+                        rhs=avg[wd][:],
+                        start=(n == 0),
+                        stop=(n == len(tiles) - 1),
+                    )
+            col = ss_col[0]
+            ss_col[0] = col + 1
             nc.scalar.activation(
-                out=junk[:], in_=cm[bk][:, :, g, :], func=ACT.Square, accum_out=ss[:, c : c + 1]
+                out=junk[:, :, 0:wd],
+                in_=cm[bank][:, :, c0 : c0 + wd],
+                func=ACT.Square,
+                accum_out=ss[:, col : col + 1],
             )
 
-        tot_ps = psum.tile([P, NCH], F32, tag="xt", name="tot_ps")
-        nc.tensor.matmul(out=tot_ps[:], lhsT=ones[:], rhs=ss[:], start=True, stop=True)
-        tot = const.tile([P, 1], F32, name="tot")
-        nc.vector.tensor_reduce(out=tot[:], in_=tot_ps[:], axis=AX.X, op=ALU.add)
-        nc.vector.tensor_scalar(out=tot[:], in0=tot[:], scalar1=EPS, scalar2=None, op0=ALU.max)
-        norm = const.tile([P, 1], F32, name="norm")
-        nc.scalar.activation(out=norm[:], in_=tot[:], func=ACT.Sqrt)
-        rnorm = const.tile([P, 1], F32, name="rnorm")
-        nc.vector.reciprocal(out=rnorm[:], in_=norm[:])
-
-        cent = data.tile([P, SPK * 4], BF16, name="cent", align_bytes=64)
-        cq = data.tile([P, SPK], U32, name="cq", align_bytes=64)
-        cs = data.tile([P, SPK], U8, name="cs", align_bytes=64)
-        centv = cent[:].rearrange("q (g k i t) -> q k g i t", g=4, k=4, i=32, t=4)
-        for bk in range(4):
-            src = cm[bk][:].rearrange("q t g i -> q g i t")
-            if bk % 2 == 0:
-                nc.vector.tensor_scalar(
-                    out=centv[:, bk], in0=src, scalar1=rnorm[:, 0:1], scalar2=None, op0=ALU.mult
-                )
-            else:
-                nc.scalar.activation(out=centv[:, bk], in_=src, func=ACT.Copy, scale=rnorm[:, 0:1])
-        nc.vector.quantize_mx(out=cq[:].bitcast(FP8X4), scales=cs[:], in_=cent[:])
-
+        grp = []
         xq = []
         xs = []
-        grp = []
-
-        def quantise(c):
-            nc.vector.quantize_mx(out=xq[c][:].bitcast(FP8X4), scales=xs[c][:], in_=grp[c][:])
-
         for c in range(NCH):
-            xw = x[c][:].bitcast(F32)
-            xt = psum.tile([P, 2, 2, P], F32, tag="xt", name="xt")
-            for j in range(2):
-                for u in range(2):
-                    nc.tensor.transpose(
-                        xt[:, j, u, :], xw[:, 256 * j + P * u : 256 * j + P * (u + 1)], ident[:]
-                    )
             gc = data.tile([P, 2 * P * 4], BF16, name="g%d" % c, align_bytes=64)
             grp.append(gc)
             xqc = data.tile([P, 2 * P], U32, name="xq%d" % c, align_bytes=64)
             xq.append(xqc)
             xsc = data.tile([P, 2 * P], U8, name="xs%d" % c, align_bytes=64)
             xs.append(xsc)
-            dst = gc[:].bitcast(F32).rearrange("q (j r u) -> q j r u", j=2, r=P, u=2)
-            srcx = xt[:].rearrange("q j u r -> q j r u")
-            if c % 8 in (1, 4, 6):
+        xts = {}
+
+        def transposes(c):
+            xw = x[c // 2][:].bitcast(F32)
+            xt = psum.tile([P, 2, 2, P], F32, tag="wk", name="xt")
+            xts[c] = xt
+            for jj in range(2):
+                for u2 in range(2):
+                    c0 = 256 * (2 * (c % 2) + jj) + P * u2
+                    nc.tensor.transpose(xt[:, jj, u2, :], xw[:, c0 : c0 + P], ident[:])
+
+        def copy_out(c, eng):
+            dst = grp[c][:].bitcast(F32).rearrange("q (j r u) -> q j r u", j=2, r=P, u=2)
+            srcx = xts[c][:].rearrange("q j u r -> q j r u")
+            if eng == "V":
                 nc.vector.tensor_copy(out=dst, in_=srcx)
             else:
                 nc.scalar.copy(out=dst, in_=srcx)
-            if c > 0:
-                quantise(c - 1)
-        quantise(NCH - 1)
 
+        def quantise(c):
+            nc.vector.quantize_mx(out=xq[c][:].bitcast(FP8X4), scales=xs[c][:], in_=grp[c][:])
+
+        tot = const.tile([P, 1], F32, name="tot")
+        norm = const.tile([P, 1], F32, name="norm")
+        rnorm = const.tile([P, 1], F32, name="rnorm")
+        cent = data.tile([P, SPK * 4], BF16, name="cent", align_bytes=64)
+        cq = data.tile([P, SPK], U32, name="cq", align_bytes=64)
+        cs = data.tile([P, SPK], U8, name="cs", align_bytes=64)
+        cent64 = cent[:].rearrange("q (g r i t) -> q r g i t", g=2, r=4, i=64, t=4)
+        cent32 = cent[:].rearrange("q (v r i t) -> q r v i t", v=4, r=4, i=32, t=4)
+        tot_ps = {}
+
+        def total():
+            tp = psum.tile([P, NSS], F32, tag="wk", name="tot_ps")
+            tot_ps[0] = tp
+            nc.tensor.matmul(out=tp[:], lhsT=ones[:], rhs=ss[:], start=True, stop=True)
+
+        def reduce_total():
+            nc.vector.tensor_reduce(out=tot[:], in_=tot_ps[0][:], axis=AX.X, op=ALU.add)
+            nc.vector.tensor_scalar(out=tot[:], in0=tot[:], scalar1=EPS, scalar2=None, op0=ALU.max)
+
+        def scale_bank(bk, eng):
+            if bk in (0, 3):
+                dst = cent64[:, 0 if bk == 0 else 2]
+                srcc = cm[bk][:].rearrange("q t (g i) -> q g i t", g=2)
+            else:
+                dst = cent32[:, 1 + bk]
+                srcc = cm[bk][:].rearrange("q t (v i) -> q v i t", v=4)
+            if eng == "V":
+                nc.vector.tensor_scalar(out=dst, in0=srcc, scalar1=rnorm[:, 0:1], scalar2=None, op0=ALU.mult)
+            else:
+                nc.scalar.activation(out=dst, in_=srcc, func=ACT.Copy, scale=rnorm[:, 0:1])
+
+        o_tiles = []
         for c in range(NCH):
             oc = data.tile([P, 2, SPK], F32, name="o%d" % c)
-            for j in range(2):
-                acc = psum.tile([P, SPK], F32, tag="cm", name="acc")
-                nc.tensor.matmul_mx(
-                    out=acc[:],
-                    lhsT=xq[c][:, P * j : P * (j + 1)].bitcast(FP8X4),
-                    lhsT_scale=xs[c][:, P * j : P * (j + 1)],
-                    rhs=cq[:].bitcast(FP8X4),
-                    rhs_scale=cs[:],
-                    start=True,
-                    stop=True,
+            o_tiles.append(oc)
+        accs = {}
+
+        def mx(i):
+            c, j = i // 2, i % 2
+            acc = psum.tile([P, SPK], F32, tag="cm", name="acc")
+            accs[i] = acc
+            nc.tensor.matmul_mx(
+                out=acc[:],
+                lhsT=xq[c][:, P * j : P * (j + 1)].bitcast(FP8X4),
+                lhsT_scale=xs[c][:, P * j : P * (j + 1)],
+                rhs=cq[:].bitcast(FP8X4),
+                rhs_scale=cs[:],
+                start=True,
+                stop=True,
+            )
+
+        def affine(i, eng):
+            dst = o_tiles[i // 2][:, i % 2, :]
+            if eng == "V":
+                nc.vector.tensor_scalar(
+                    out=dst, in0=accs[i][:], scalar1=absw[:, 0:1], scalar2=bias[:, 0:1], op0=ALU.mult, op1=ALU.add
                 )
-                if (2 * c + j) % 4 == 3:
-                    nc.vector.tensor_scalar(
-                        out=oc[:, j, :],
-                        in0=acc[:],
-                        scalar1=absw[:, 0:1],
-                        scalar2=bias[:, 0:1],
-                        op0=ALU.mult,
-                        op1=ALU.add,
-                    )
-                else:
-                    nc.scalar.activation(
-                        out=oc[:, j, :], in_=acc[:], func=ACT.Relu, scale=absw[:, 0:1], bias=bias[:, 0:1]
-                    )
-            nc.vector.tensor_scalar(
-                out=oc[:], in0=oc[:], scalar1=0.0, scalar2=1.0, op0=ALU.max, op1=ALU.min
-            )
-            nc.sync.dma_start(
-                out=out[CH_ROWS * c : CH_ROWS * (c + 1), :].rearrange("(p j) n -> p j n", j=2),
-                in_=oc[:],
-            )
+            else:
+                nc.scalar.activation(
+                    out=dst, in_=accs[i][:], func=ACT.Relu, scale=absw[:, 0:1], bias=bias[:, 0:1]
+                )
+
+        def clip(ap):
+            nc.vector.tensor_scalar(out=ap, in0=ap, scalar1=0.0, scalar2=1.0, op0=ALU.max, op1=ALU.min)
+
+        def out_view(c):
+            u, h2 = c // 2, c % 2
+            if u % 2 == 0:
+                return out[512 * u : 512 * (u + 1), :].rearrange("(p a) n -> p a n", a=4)[:, 2 * h2 : 2 * h2 + 2, :]
+            r0 = 512 * u + 256 * h2
+            return out[r0 : r0 + 256, :].rearrange("(p j) n -> p j n", j=2)
+
+        for u in range(NU):
+            if u % 2 == 0:
+                means(u, 0)
+            else:
+                means(u, 0)
+                means(u, 1)
+            if u == 3:
+                scale_and_bias()
+            if 1 <= u <= 6:
+                for c in (2 * u - 2, 2 * u - 1):
+                    transposes(c)
+                    copy_out(c, "V" if c % 4 == 3 else "A")
+                    if c >= 1:
+                        quantise(c - 1)
+        transposes(12)
+        copy_out(12, "A")
+        total()
+        transposes(13)
+        transposes(14)
+        transposes(15)
+        reduce_total()
+        quantise(11)
+        nc.scalar.activation(out=norm[:], in_=tot[:], func=ACT.Sqrt)
+        nc.vector.reciprocal(out=rnorm[:], in_=norm[:])
+        scale_bank(0, "V")
+        scale_bank(1, "A")
+        scale_bank(3, "V")
+        scale_bank(2, "A")
+        nc.vector.quantize_mx(out=cq[:].bitcast(FP8X4), scales=cs[:], in_=cent[:])
+
+        mx(0)
+        mx(1)
+        affine(0, "A")
+        affine(1, "V")
+        for j in range(2):
+            clip(o_tiles[0][:, j, :])
+            nc.sync.dma_start(out=out_view(0)[:, j, :], in_=o_tiles[0][:, j, :])
+        quantise(12)
+        for c in range(1, NCH):
+            mx(2 * c)
+            mx(2 * c + 1)
+            affine(2 * c, "A")
+            affine(2 * c + 1, "V" if c % 2 == 1 else "A")
+            clip(o_tiles[c][:])
+            nc.sync.dma_start(out=out_view(c), in_=o_tiles[c][:])
+            if c in (1, 3, 5):
+                copy_out(13 + (c - 1) // 2, "A")
+            if c in (2, 4, 6):
+                quantise(13 + (c - 2) // 2)

@@ -48,6 +48,22 @@ def tile_similaritymatrixlayer_kernel(tc, inputs, w, b, out):
         nc.scalar.dma_start(out=w16[:], in_=w.partition_broadcast(P))
         nc.scalar.dma_start(out=b16[:], in_=b.partition_broadcast(P))
 
+        zb = data.tile([P, 1024], BF16, name="zb", align_bytes=64)
+        zq = data.tile([P, 256], U32, name="zq", align_bytes=64)
+        zs = data.tile([P, 256], U8, name="zs", align_bytes=64)
+        nc.vector.memset(zb[:], 1.0)
+        nc.vector.quantize_mx(out=zq[:].bitcast(FP8X4), scales=zs[:], in_=zb[:])
+        zp = psum.tile([P, 256], F32, tag="wk", name="zp")
+        for n in range(8):
+            nc.tensor.matmul_mx(
+                out=zp[:],
+                lhsT=zq[:, 0:P].bitcast(FP8X4),
+                lhsT_scale=zs[:, 0:P],
+                rhs=zq[:].bitcast(FP8X4),
+                rhs_scale=zs[:],
+                start=True,
+                stop=True,
+            )
         warm = const.tile([P, 1], F32, name="warm")
         nc.vector.memset(warm[:], 1.0)
         nc.scalar.activation(out=warm[:], in_=warm[:], func=ACT.Sqrt)

@@ -1,3 +1,4 @@
+import math
 from contextlib import ExitStack
 
 import concourse.mybir as mybir
@@ -18,7 +19,6 @@ K = 512
 SPK = 512
 EPS = 1e-6
 NU = 8
-NCH = 16
 FLOPS = 2 * ROWS * K * SPK
 
 
@@ -48,22 +48,6 @@ def tile_similaritymatrixlayer_kernel(tc, inputs, w, b, out):
         nc.scalar.dma_start(out=w16[:], in_=w.partition_broadcast(P))
         nc.scalar.dma_start(out=b16[:], in_=b.partition_broadcast(P))
 
-        zb = data.tile([P, 1024], BF16, name="zb", align_bytes=64)
-        zq = data.tile([P, 256], U32, name="zq", align_bytes=64)
-        zs = data.tile([P, 256], U8, name="zs", align_bytes=64)
-        nc.vector.memset(zb[:], 1.0)
-        nc.vector.quantize_mx(out=zq[:].bitcast(FP8X4), scales=zs[:], in_=zb[:])
-        zp = psum.tile([P, 256], F32, tag="wk", name="zp")
-        for n in range(8):
-            nc.tensor.matmul_mx(
-                out=zp[:],
-                lhsT=zq[:, 0:P].bitcast(FP8X4),
-                lhsT_scale=zs[:, 0:P],
-                rhs=zq[:].bitcast(FP8X4),
-                rhs_scale=zs[:],
-                start=True,
-                stop=True,
-            )
         warm = const.tile([P, 1], F32, name="warm")
         nc.vector.memset(warm[:], 1.0)
         nc.scalar.activation(out=warm[:], in_=warm[:], func=ACT.Sqrt)
@@ -92,49 +76,48 @@ def tile_similaritymatrixlayer_kernel(tc, inputs, w, b, out):
             nc.vector.tensor_tensor(out=absw[:], in0=wf[:], in1=negw[:], op=ALU.max)
             nc.vector.tensor_copy(out=bias[:], in_=b16[:])
 
-        cm = []
-        for bk in range(4):
-            cmb = psum.tile([P, 4, P], F32, tag="cm", name="cm%d" % bk)
-            cm.append(cmb)
         NSS = 12
         ss = const.tile([P, NSS], F32, name="ss")
         junk = const.tile([P, 4, 64], F32, name="junk")
-        ss_col = [0]
+        cms = data.tile([P, SPK, 4], F32, name="cms")
+        cmr = {}
+        order_of = {}
+
+        def width(u):
+            return 64 if u % 2 == 0 else 32
 
         def means(u, h):
             xv = x[u][:].rearrange("p (a u q e) -> p a u e q", a=4, u=2, q=P, e=2)
-            if u % 2 == 0:
-                bank, c0, wd, tiles = (0 if u % 4 == 0 else 3), 64 * (u // 4), 64, (0, 1, 2, 3)
-            else:
-                bank, c0, wd, tiles = 1 + h, 32 * (u // 2), 32, (2 * h, 2 * h + 1)
+            wd = width(u)
+            tiles = (0, 1, 2, 3) if u % 2 == 0 else (2 * h, 2 * h + 1)
+            reg = psum.tile([P, 4, wd], F32, tag="cm", name="cmr")
+            cmr[(u, h)] = reg
+            order_of[(u, h)] = len(order_of)
             for t in range(4):
                 for n, a in enumerate(tiles):
                     nc.tensor.matmul(
-                        out=cm[bank][:, t, c0 : c0 + wd],
+                        out=reg[:, t, :],
                         lhsT=xv[:, a, t // 2, t % 2, :],
                         rhs=avg[wd][:],
                         start=(n == 0),
                         stop=(n == len(tiles) - 1),
                     )
-            col = ss_col[0]
-            ss_col[0] = col + 1
+
+        def square(u, h):
+            col = order_of[(u, h)]
             nc.scalar.activation(
-                out=junk[:, :, 0:wd],
-                in_=cm[bank][:, :, c0 : c0 + wd],
-                func=ACT.Square,
-                accum_out=ss[:, col : col + 1],
+                out=junk[:, :, 0 : width(u)], in_=cmr[(u, h)][:], func=ACT.Square, accum_out=ss[:, col : col + 1]
             )
 
-        grp = []
-        xq = []
-        xs = []
-        for c in range(NCH):
-            gc = data.tile([P, 2 * P * 4], BF16, name="g%d" % c, align_bytes=64)
-            grp.append(gc)
-            xqc = data.tile([P, 2 * P], U32, name="xq%d" % c, align_bytes=64)
-            xq.append(xqc)
-            xsc = data.tile([P, 2 * P], U8, name="xs%d" % c, align_bytes=64)
-            xs.append(xsc)
+        def keep_means(u, h):
+            s0 = 64 * u + 32 * h
+            nc.vector.tensor_copy(
+                out=cms[:, s0 : s0 + width(u), :], in_=cmr[(u, h)][:].rearrange("q t s -> q s t")
+            )
+
+        grp = {}
+        xq = {}
+        xs = {}
         xts = {}
 
         def transposes(c):
@@ -147,7 +130,9 @@ def tile_similaritymatrixlayer_kernel(tc, inputs, w, b, out):
                     nc.tensor.transpose(xt[:, jj, u2, :], xw[:, c0 : c0 + P], ident[:])
 
         def copy_out(c, eng):
-            dst = grp[c][:].bitcast(F32).rearrange("q (j r u) -> q j r u", j=2, r=P, u=2)
+            gc = data.tile([P, 2 * P * 4], BF16, name="g%d" % c, align_bytes=64)
+            grp[c] = gc
+            dst = gc[:].bitcast(F32).rearrange("q (j r u) -> q j r u", j=2, r=P, u=2)
             srcx = xts[c][:].rearrange("q j u r -> q j r u")
             if eng == "V":
                 nc.vector.tensor_copy(out=dst, in_=srcx)
@@ -155,43 +140,58 @@ def tile_similaritymatrixlayer_kernel(tc, inputs, w, b, out):
                 nc.scalar.copy(out=dst, in_=srcx)
 
         def quantise(c):
-            nc.vector.quantize_mx(out=xq[c][:].bitcast(FP8X4), scales=xs[c][:], in_=grp[c][:])
+            xqc = data.tile([P, 2 * P], U32, name="xq%d" % c, align_bytes=64)
+            xq[c] = xqc
+            xsc = data.tile([P, 2 * P], U8, name="xs%d" % c, align_bytes=64)
+            xs[c] = xsc
+            nc.vector.quantize_mx(out=xqc[:].bitcast(FP8X4), scales=xsc[:], in_=grp[c][:])
 
-        tot = const.tile([P, 1], F32, name="tot")
+        part = const.tile([P, 1], F32, name="part")
         norm = const.tile([P, 1], F32, name="norm")
         rnorm = const.tile([P, 1], F32, name="rnorm")
+        tot_ps = {}
+
+        def partial_total():
+            nc.vector.tensor_reduce(out=part[:], in_=ss[:, 0 : NSS - 1], axis=AX.X, op=ALU.add)
+
+        def total(step):
+            if step == 0:
+                tp = psum.tile([P, 1], F32, tag="cm", name="tot_ps")
+                tot_ps[0] = tp
+                nc.tensor.matmul(out=tp[:], lhsT=ones[:], rhs=part[:], start=True, stop=False)
+            else:
+                nc.tensor.matmul(out=tot_ps[0][:], lhsT=ones[:], rhs=ss[:, NSS - 1 : NSS], start=False, stop=True)
+
+        def root():
+            nc.scalar.activation(out=norm[:], in_=tot_ps[0][:], func=ACT.Sqrt)
+
+        def inverse():
+            nc.vector.tensor_scalar(out=norm[:], in0=norm[:], scalar1=math.sqrt(EPS), scalar2=None, op0=ALU.max)
+            nc.vector.reciprocal(out=rnorm[:], in_=norm[:])
+
         cent = data.tile([P, SPK * 4], BF16, name="cent", align_bytes=64)
         cq = data.tile([P, SPK], U32, name="cq", align_bytes=64)
         cs = data.tile([P, SPK], U8, name="cs", align_bytes=64)
-        cent64 = cent[:].rearrange("q (g r i t) -> q r g i t", g=2, r=4, i=64, t=4)
-        cent32 = cent[:].rearrange("q (v r i t) -> q r v i t", v=4, r=4, i=32, t=4)
-        tot_ps = {}
+        cms_flat = cms[:].rearrange("q s t -> q (s t)")
+        HALF = SPK * 2
 
-        def total():
-            tp = psum.tile([P, NSS], F32, tag="wk", name="tot_ps")
-            tot_ps[0] = tp
-            nc.tensor.matmul(out=tp[:], lhsT=ones[:], rhs=ss[:], start=True, stop=True)
-
-        def reduce_total():
-            nc.vector.tensor_reduce(out=tot[:], in_=tot_ps[0][:], axis=AX.X, op=ALU.add)
-            nc.vector.tensor_scalar(out=tot[:], in0=tot[:], scalar1=EPS, scalar2=None, op0=ALU.max)
-
-        def scale_bank(bk, eng):
-            if bk in (0, 3):
-                dst = cent64[:, 0 if bk == 0 else 2]
-                srcc = cm[bk][:].rearrange("q t (g i) -> q g i t", g=2)
-            else:
-                dst = cent32[:, 1 + bk]
-                srcc = cm[bk][:].rearrange("q t (v i) -> q v i t", v=4)
+        def scale_centroids(half, eng):
+            cols = slice(HALF * half, HALF * (half + 1))
             if eng == "V":
-                nc.vector.tensor_scalar(out=dst, in0=srcc, scalar1=rnorm[:, 0:1], scalar2=None, op0=ALU.mult)
+                nc.vector.tensor_scalar(
+                    out=cent[:, cols], in0=cms_flat[:, cols], scalar1=rnorm[:, 0:1], scalar2=None, op0=ALU.mult
+                )
             else:
-                nc.scalar.activation(out=dst, in_=srcc, func=ACT.Copy, scale=rnorm[:, 0:1])
+                nc.scalar.activation(out=cent[:, cols], in_=cms_flat[:, cols], func=ACT.Copy, scale=rnorm[:, 0:1])
 
-        o_tiles = []
-        for c in range(NCH):
-            oc = data.tile([P, 2, SPK], F32, name="o%d" % c)
-            o_tiles.append(oc)
+        def quantise_centroids(half):
+            nc.vector.quantize_mx(
+                out=cq[:, 256 * half : 256 * (half + 1)].bitcast(FP8X4),
+                scales=cs[:, 256 * half : 256 * (half + 1)],
+                in_=cent[:, HALF * half : HALF * (half + 1)],
+            )
+
+        o_tiles = {}
         accs = {}
 
         def mx(i):
@@ -209,6 +209,9 @@ def tile_similaritymatrixlayer_kernel(tc, inputs, w, b, out):
             )
 
         def affine(i, eng):
+            if i % 2 == 0:
+                oc = data.tile([P, 2, SPK], F32, name="o%d" % (i // 2))
+                o_tiles[i // 2] = oc
             dst = o_tiles[i // 2][:, i % 2, :]
             if eng == "V":
                 nc.vector.tensor_scalar(
@@ -229,52 +232,197 @@ def tile_similaritymatrixlayer_kernel(tc, inputs, w, b, out):
             r0 = 512 * u + 256 * h2
             return out[r0 : r0 + 256, :].rearrange("(p j) n -> p j n", j=2)
 
-        for u in range(NU):
-            if u % 2 == 0:
-                means(u, 0)
-            else:
-                means(u, 0)
-                means(u, 1)
-            if u == 3:
-                scale_and_bias()
-            if 1 <= u <= 6:
-                for c in (2 * u - 2, 2 * u - 1):
-                    transposes(c)
-                    copy_out(c, "V" if c % 4 == 3 else "A")
-                    if c >= 1:
-                        quantise(c - 1)
-        transposes(12)
-        copy_out(12, "A")
-        total()
-        transposes(13)
-        transposes(14)
-        transposes(15)
-        reduce_total()
-        quantise(11)
-        nc.scalar.activation(out=norm[:], in_=tot[:], func=ACT.Sqrt)
-        nc.vector.reciprocal(out=rnorm[:], in_=norm[:])
-        scale_bank(0, "V")
-        scale_bank(1, "A")
-        scale_bank(3, "V")
-        scale_bank(2, "A")
-        nc.vector.quantize_mx(out=cq[:].bitcast(FP8X4), scales=cs[:], in_=cent[:])
-
+        means(0, 0)
+        square(0, 0)
+        keep_means(0, 0)
+        means(1, 0)
+        square(1, 0)
+        keep_means(1, 0)
+        means(1, 1)
+        square(1, 1)
+        keep_means(1, 1)
+        transposes(0)
+        copy_out(0, "V")
+        means(2, 0)
+        square(2, 0)
+        keep_means(2, 0)
+        transposes(1)
+        copy_out(1, "V")
+        quantise(0)
+        means(3, 0)
+        square(3, 0)
+        keep_means(3, 0)
+        means(3, 1)
+        square(3, 1)
+        keep_means(3, 1)
+        transposes(2)
+        copy_out(2, "V")
+        quantise(1)
+        means(4, 0)
+        square(4, 0)
+        keep_means(4, 0)
+        transposes(3)
+        copy_out(3, "V")
+        quantise(2)
+        scale_and_bias()
+        means(5, 0)
+        square(5, 0)
+        keep_means(5, 0)
+        means(5, 1)
+        square(5, 1)
+        keep_means(5, 1)
+        quantise(3)
+        means(6, 0)
+        square(6, 0)
+        keep_means(6, 0)
+        means(7, 0)
+        square(7, 0)
+        keep_means(7, 0)
+        partial_total()
+        means(7, 1)
+        square(7, 1)
+        keep_means(7, 1)
+        transposes(4)
+        transposes(5)
+        total(0)
+        total(1)
+        copy_out(4, "A")
+        copy_out(5, "V")
+        transposes(6)
+        transposes(7)
+        root()
+        copy_out(6, "A")
+        inverse()
+        scale_centroids(0, "V")
+        quantise_centroids(0)
+        copy_out(7, "V")
+        scale_centroids(1, "A")
+        quantise_centroids(1)
+        transposes(8)
+        transposes(9)
+        copy_out(8, "A")
+        copy_out(9, "A")
+        quantise(4)
+        quantise(5)
+        transposes(10)
+        transposes(11)
+        copy_out(10, "V")
         mx(0)
         mx(1)
         affine(0, "A")
         affine(1, "V")
-        for j in range(2):
-            clip(o_tiles[0][:, j, :])
-            nc.sync.dma_start(out=out_view(0)[:, j, :], in_=o_tiles[0][:, j, :])
+        clip(o_tiles[0][:, 0, :])
+        nc.sync.dma_start(out=out_view(0)[:, 0, :], in_=o_tiles[0][:, 0, :])
+        clip(o_tiles[0][:, 1, :])
+        nc.sync.dma_start(out=out_view(0)[:, 1, :], in_=o_tiles[0][:, 1, :])
+        quantise(6)
+        mx(2)
+        mx(3)
+        affine(2, "A")
+        affine(3, "A")
+        clip(o_tiles[1][:])
+        nc.sync.dma_start(out=out_view(1), in_=o_tiles[1][:])
+        quantise(7)
+        copy_out(11, "A")
+        transposes(12)
+        transposes(13)
+        mx(4)
+        mx(5)
+        affine(4, "A")
+        affine(5, "V")
+        clip(o_tiles[2][:])
+        nc.sync.dma_start(out=out_view(2), in_=o_tiles[2][:])
+        quantise(8)
+        mx(6)
+        mx(7)
+        affine(6, "A")
+        affine(7, "A")
+        clip(o_tiles[3][:])
+        nc.sync.dma_start(out=out_view(3), in_=o_tiles[3][:])
+        quantise(9)
+        copy_out(12, "A")
+        mx(8)
+        mx(9)
+        affine(8, "A")
+        affine(9, "V")
+        clip(o_tiles[4][:])
+        nc.sync.dma_start(out=out_view(4), in_=o_tiles[4][:])
+        quantise(10)
+        copy_out(13, "A")
+        transposes(14)
+        transposes(15)
+        mx(10)
+        mx(11)
+        affine(10, "A")
+        affine(11, "A")
+        clip(o_tiles[5][:])
+        nc.sync.dma_start(out=out_view(5), in_=o_tiles[5][:])
+        quantise(11)
+        mx(12)
+        mx(13)
+        affine(12, "A")
+        affine(13, "V")
+        clip(o_tiles[6][:])
+        nc.sync.dma_start(out=out_view(6), in_=o_tiles[6][:])
         quantise(12)
-        for c in range(1, NCH):
-            mx(2 * c)
-            mx(2 * c + 1)
-            affine(2 * c, "A")
-            affine(2 * c + 1, "V" if c % 2 == 1 else "A")
-            clip(o_tiles[c][:])
-            nc.sync.dma_start(out=out_view(c), in_=o_tiles[c][:])
-            if c in (1, 3, 5):
-                copy_out(13 + (c - 1) // 2, "A")
-            if c in (2, 4, 6):
-                quantise(13 + (c - 2) // 2)
+        copy_out(14, "A")
+        mx(14)
+        mx(15)
+        affine(14, "A")
+        affine(15, "A")
+        clip(o_tiles[7][:])
+        nc.sync.dma_start(out=out_view(7), in_=o_tiles[7][:])
+        quantise(13)
+        copy_out(15, "A")
+        mx(16)
+        mx(17)
+        affine(16, "A")
+        affine(17, "V")
+        clip(o_tiles[8][:])
+        nc.sync.dma_start(out=out_view(8), in_=o_tiles[8][:])
+        quantise(14)
+        mx(18)
+        mx(19)
+        affine(18, "A")
+        affine(19, "A")
+        clip(o_tiles[9][:])
+        nc.sync.dma_start(out=out_view(9), in_=o_tiles[9][:])
+        quantise(15)
+        mx(20)
+        mx(21)
+        affine(20, "A")
+        affine(21, "V")
+        clip(o_tiles[10][:])
+        nc.sync.dma_start(out=out_view(10), in_=o_tiles[10][:])
+        mx(22)
+        mx(23)
+        affine(22, "A")
+        affine(23, "A")
+        clip(o_tiles[11][:])
+        nc.sync.dma_start(out=out_view(11), in_=o_tiles[11][:])
+        mx(24)
+        mx(25)
+        affine(24, "A")
+        affine(25, "V")
+        clip(o_tiles[12][:])
+        nc.sync.dma_start(out=out_view(12), in_=o_tiles[12][:])
+        mx(26)
+        mx(27)
+        affine(26, "A")
+        affine(27, "A")
+        clip(o_tiles[13][:])
+        nc.sync.dma_start(out=out_view(13), in_=o_tiles[13][:])
+        mx(28)
+        mx(29)
+        affine(28, "A")
+        affine(29, "V")
+        clip(o_tiles[14][:])
+        nc.sync.dma_start(out=out_view(14), in_=o_tiles[14][:])
+        mx(30)
+        mx(31)
+        affine(30, "A")
+        affine(31, "V")
+        clip(o_tiles[15][:, 0, :])
+        nc.sync.dma_start(out=out_view(15)[:, 0, :], in_=o_tiles[15][:, 0, :])
+        clip(o_tiles[15][:, 1, :])
+        nc.sync.dma_start(out=out_view(15)[:, 1, :], in_=o_tiles[15][:, 1, :])

@@ -19,6 +19,7 @@ K = 512
 SPK = 512
 EPS = 1e-6
 NU = 8
+NCH = 16
 FLOPS = 2 * ROWS * K * SPK
 
 
@@ -43,10 +44,10 @@ def tile_similaritymatrixlayer_kernel(tc, inputs, w, b, out):
                         out=xu[:, 2 * K * h : 2 * K * (h + 1)],
                         in_=rows[256 * h : 256 * (h + 1), :].rearrange("(p j) k -> p (j k)", j=2),
                     )
-        w16 = const.tile([P, 1], BF16, name="w16")
-        b16 = const.tile([P, 1], BF16, name="b16")
-        nc.scalar.dma_start(out=w16[:], in_=w.partition_broadcast(P))
-        nc.scalar.dma_start(out=b16[:], in_=b.partition_broadcast(P))
+        wb16 = const.tile([P, 32], BF16, name="wb16")
+        nc.vector.memset(wb16[:], 0.0)
+        nc.scalar.dma_start(out=wb16[0:1, 0:1], in_=w.rearrange("(o n) -> o n", o=1))
+        nc.scalar.dma_start(out=wb16[0:1, 16:17], in_=b.rearrange("(o n) -> o n", o=1))
 
         warm = const.tile([P, 1], F32, name="warm")
         nc.vector.memset(warm[:], 1.0)
@@ -65,54 +66,55 @@ def tile_similaritymatrixlayer_kernel(tc, inputs, w, b, out):
         ones = const.tile([P, P], F32, name="ones")
         nc.vector.memset(ones[:], 1.0)
 
-        wf = const.tile([P, 1], F32, name="wf")
+        ones16 = const.tile([P, P], BF16, name="ones16")
+        nc.vector.memset(ones16[:], 1.0)
+        wbf = const.tile([P, 32], F32, name="wbf")
         negw = const.tile([P, 1], F32, name="negw")
         absw = const.tile([P, 1], F32, name="absw")
-        bias = const.tile([P, 1], F32, name="bias")
+        bias = wbf[:, 16:17]
+        wb_ps = {}
+
+        def spread():
+            wp = psum.tile([P, 32], F32, tag="wk", name="wb_ps")
+            wb_ps[0] = wp
+            nc.tensor.matmul(out=wp[:], lhsT=ones16[:], rhs=wb16[:], start=True, stop=True)
 
         def scale_and_bias():
-            nc.vector.tensor_copy(out=wf[:], in_=w16[:])
-            nc.vector.tensor_scalar(out=negw[:], in0=wf[:], scalar1=-1.0, scalar2=None, op0=ALU.mult)
-            nc.vector.tensor_tensor(out=absw[:], in0=wf[:], in1=negw[:], op=ALU.max)
-            nc.vector.tensor_copy(out=bias[:], in_=b16[:])
+            nc.vector.tensor_copy(out=wbf[:], in_=wb_ps[0][:])
+            nc.vector.tensor_scalar(out=negw[:], in0=wbf[:, 0:1], scalar1=-1.0, scalar2=None, op0=ALU.mult)
+            nc.vector.tensor_tensor(out=absw[:], in0=wbf[:, 0:1], in1=negw[:], op=ALU.max)
 
+        cm = []
+        for bk in range(4):
+            cmb = psum.tile([P, 4, P], F32, tag="cm", name="cm%d" % bk)
+            cm.append(cmb)
         NSS = 12
         ss = const.tile([P, NSS], F32, name="ss")
         junk = const.tile([P, 4, 64], F32, name="junk")
-        cms = data.tile([P, SPK, 4], F32, name="cms")
-        cmr = {}
-        order_of = {}
-
-        def width(u):
-            return 64 if u % 2 == 0 else 32
+        ss_col = [0]
 
         def means(u, h):
             xv = x[u][:].rearrange("p (a u q e) -> p a u e q", a=4, u=2, q=P, e=2)
-            wd = width(u)
-            tiles = (0, 1, 2, 3) if u % 2 == 0 else (2 * h, 2 * h + 1)
-            reg = psum.tile([P, 4, wd], F32, tag="cm", name="cmr")
-            cmr[(u, h)] = reg
-            order_of[(u, h)] = len(order_of)
+            if u % 2 == 0:
+                bank, c0, wd, tiles = (0 if u % 4 == 0 else 3), 64 * (u // 4), 64, (0, 1, 2, 3)
+            else:
+                bank, c0, wd, tiles = 1 + h, 32 * (u // 2), 32, (2 * h, 2 * h + 1)
             for t in range(4):
                 for n, a in enumerate(tiles):
                     nc.tensor.matmul(
-                        out=reg[:, t, :],
+                        out=cm[bank][:, t, c0 : c0 + wd],
                         lhsT=xv[:, a, t // 2, t % 2, :],
                         rhs=avg[wd][:],
                         start=(n == 0),
                         stop=(n == len(tiles) - 1),
                     )
-
-        def square(u, h):
-            col = order_of[(u, h)]
+            col = ss_col[0]
+            ss_col[0] = col + 1
             nc.scalar.activation(
-                out=junk[:, :, 0 : width(u)], in_=cmr[(u, h)][:], func=ACT.Square, accum_out=ss[:, col : col + 1]
-            )
-
-        def keep_means(u, h):
-            s0 = 64 * u + 32 * h
-            nc.vector.tensor_copy(
-                out=cms[:, s0 : s0 + width(u), :], in_=cmr[(u, h)][:].rearrange("q t s -> q s t")
+                out=junk[:, :, 0:wd],
+                in_=cm[bank][:, :, c0 : c0 + wd],
+                func=ACT.Square,
+                accum_out=ss[:, col : col + 1],
             )
 
         grp = {}
@@ -132,7 +134,7 @@ def tile_similaritymatrixlayer_kernel(tc, inputs, w, b, out):
         def copy_out(c, eng):
             gc = data.tile([P, 2 * P * 4], BF16, name="g%d" % c, align_bytes=64)
             grp[c] = gc
-            dst = gc[:].bitcast(F32).rearrange("q (j r u) -> q j r u", j=2, r=P, u=2)
+            dst = grp[c][:].bitcast(F32).rearrange("q (j r u) -> q j r u", j=2, r=P, u=2)
             srcx = xts[c][:].rearrange("q j u r -> q j r u")
             if eng == "V":
                 nc.vector.tensor_copy(out=dst, in_=srcx)
@@ -144,19 +146,25 @@ def tile_similaritymatrixlayer_kernel(tc, inputs, w, b, out):
             xq[c] = xqc
             xsc = data.tile([P, 2 * P], U8, name="xs%d" % c, align_bytes=64)
             xs[c] = xsc
-            nc.vector.quantize_mx(out=xqc[:].bitcast(FP8X4), scales=xsc[:], in_=grp[c][:])
+            nc.vector.quantize_mx(out=xq[c][:].bitcast(FP8X4), scales=xs[c][:], in_=grp[c][:])
 
-        part = const.tile([P, 1], F32, name="part")
         norm = const.tile([P, 1], F32, name="norm")
         rnorm = const.tile([P, 1], F32, name="rnorm")
+        cent = data.tile([P, SPK * 4], BF16, name="cent", align_bytes=64)
+        cq = data.tile([P, SPK], U32, name="cq", align_bytes=64)
+        cs = data.tile([P, SPK], U8, name="cs", align_bytes=64)
+        cent64 = cent[:].rearrange("q (g r i t) -> q r g i t", g=2, r=4, i=64, t=4)
+        cent32 = cent[:].rearrange("q (v r i t) -> q r v i t", v=4, r=4, i=32, t=4)
         tot_ps = {}
+
+        part = const.tile([P, 1], F32, name="part")
 
         def partial_total():
             nc.vector.tensor_reduce(out=part[:], in_=ss[:, 0 : NSS - 1], axis=AX.X, op=ALU.add)
 
         def total(step):
             if step == 0:
-                tp = psum.tile([P, 1], F32, tag="cm", name="tot_ps")
+                tp = psum.tile([P, 1], F32, tag="wk", name="tot_ps")
                 tot_ps[0] = tp
                 nc.tensor.matmul(out=tp[:], lhsT=ones[:], rhs=part[:], start=True, stop=False)
             else:
@@ -169,27 +177,17 @@ def tile_similaritymatrixlayer_kernel(tc, inputs, w, b, out):
             nc.vector.tensor_scalar(out=norm[:], in0=norm[:], scalar1=math.sqrt(EPS), scalar2=None, op0=ALU.max)
             nc.vector.reciprocal(out=rnorm[:], in_=norm[:])
 
-        cent = data.tile([P, SPK * 4], BF16, name="cent", align_bytes=64)
-        cq = data.tile([P, SPK], U32, name="cq", align_bytes=64)
-        cs = data.tile([P, SPK], U8, name="cs", align_bytes=64)
-        cms_flat = cms[:].rearrange("q s t -> q (s t)")
-        HALF = SPK * 2
-
-        def scale_centroids(half, eng):
-            cols = slice(HALF * half, HALF * (half + 1))
-            if eng == "V":
-                nc.vector.tensor_scalar(
-                    out=cent[:, cols], in0=cms_flat[:, cols], scalar1=rnorm[:, 0:1], scalar2=None, op0=ALU.mult
-                )
+        def scale_bank(bk, eng):
+            if bk in (0, 3):
+                dst = cent64[:, 0 if bk == 0 else 2]
+                srcc = cm[bk][:].rearrange("q t (g i) -> q g i t", g=2)
             else:
-                nc.scalar.activation(out=cent[:, cols], in_=cms_flat[:, cols], func=ACT.Copy, scale=rnorm[:, 0:1])
-
-        def quantise_centroids(half):
-            nc.vector.quantize_mx(
-                out=cq[:, 256 * half : 256 * (half + 1)].bitcast(FP8X4),
-                scales=cs[:, 256 * half : 256 * (half + 1)],
-                in_=cent[:, HALF * half : HALF * (half + 1)],
-            )
+                dst = cent32[:, 1 + bk]
+                srcc = cm[bk][:].rearrange("q t (v i) -> q v i t", v=4)
+            if eng == "V":
+                nc.vector.tensor_scalar(out=dst, in0=srcc, scalar1=rnorm[:, 0:1], scalar2=None, op0=ALU.mult)
+            else:
+                nc.scalar.activation(out=dst, in_=srcc, func=ACT.Copy, scale=rnorm[:, 0:1])
 
         o_tiles = {}
         accs = {}
@@ -215,11 +213,11 @@ def tile_similaritymatrixlayer_kernel(tc, inputs, w, b, out):
             dst = o_tiles[i // 2][:, i % 2, :]
             if eng == "V":
                 nc.vector.tensor_scalar(
-                    out=dst, in0=accs[i][:], scalar1=absw[:, 0:1], scalar2=bias[:, 0:1], op0=ALU.mult, op1=ALU.add
+                    out=dst, in0=accs[i][:], scalar1=absw[:, 0:1], scalar2=bias, op0=ALU.mult, op1=ALU.add
                 )
             else:
                 nc.scalar.activation(
-                    out=dst, in_=accs[i][:], func=ACT.Relu, scale=absw[:, 0:1], bias=bias[:, 0:1]
+                    out=dst, in_=accs[i][:], func=ACT.Relu, scale=absw[:, 0:1], bias=bias
                 )
 
         def clip(ap):
@@ -232,197 +230,55 @@ def tile_similaritymatrixlayer_kernel(tc, inputs, w, b, out):
             r0 = 512 * u + 256 * h2
             return out[r0 : r0 + 256, :].rearrange("(p j) n -> p j n", j=2)
 
-        means(0, 0)
-        square(0, 0)
-        keep_means(0, 0)
-        means(1, 0)
-        square(1, 0)
-        keep_means(1, 0)
-        means(1, 1)
-        square(1, 1)
-        keep_means(1, 1)
-        transposes(0)
-        copy_out(0, "V")
-        means(2, 0)
-        square(2, 0)
-        keep_means(2, 0)
-        transposes(1)
-        copy_out(1, "V")
-        quantise(0)
-        means(3, 0)
-        square(3, 0)
-        keep_means(3, 0)
-        means(3, 1)
-        square(3, 1)
-        keep_means(3, 1)
-        transposes(2)
-        copy_out(2, "V")
-        quantise(1)
-        means(4, 0)
-        square(4, 0)
-        keep_means(4, 0)
-        transposes(3)
-        copy_out(3, "V")
-        quantise(2)
-        scale_and_bias()
-        means(5, 0)
-        square(5, 0)
-        keep_means(5, 0)
-        means(5, 1)
-        square(5, 1)
-        keep_means(5, 1)
-        quantise(3)
-        means(6, 0)
-        square(6, 0)
-        keep_means(6, 0)
-        means(7, 0)
-        square(7, 0)
-        keep_means(7, 0)
-        partial_total()
-        means(7, 1)
-        square(7, 1)
-        keep_means(7, 1)
-        transposes(4)
-        transposes(5)
+        for u in range(NU):
+            means(u, 0)
+            if u == 7:
+                partial_total()
+            if u % 2 == 1:
+                means(u, 1)
+            if u == 2:
+                spread()
+            if u == 3:
+                scale_and_bias()
+            if 1 <= u <= 6:
+                for c in (2 * u - 2, 2 * u - 1):
+                    transposes(c)
+                    copy_out(c, "V" if c % 4 == 3 else "A")
+                    if c >= 1:
+                        quantise(c - 1)
+        transposes(12)
         total(0)
         total(1)
-        copy_out(4, "A")
-        copy_out(5, "V")
-        transposes(6)
-        transposes(7)
+        transposes(13)
+        transposes(14)
         root()
-        copy_out(6, "A")
+        transposes(15)
+        quantise(11)
         inverse()
-        scale_centroids(0, "V")
-        quantise_centroids(0)
-        copy_out(7, "V")
-        scale_centroids(1, "A")
-        quantise_centroids(1)
-        transposes(8)
-        transposes(9)
-        copy_out(8, "A")
-        copy_out(9, "A")
-        quantise(4)
-        quantise(5)
-        transposes(10)
-        transposes(11)
-        copy_out(10, "V")
+        scale_bank(0, "V")
+        scale_bank(1, "A")
+        scale_bank(3, "V")
+        scale_bank(2, "A")
+        nc.vector.quantize_mx(out=cq[:].bitcast(FP8X4), scales=cs[:], in_=cent[:])
+        copy_out(12, "A")
+        copy_out(13, "A")
+        quantise(12)
+
         mx(0)
         mx(1)
-        affine(0, "A")
-        affine(1, "V")
-        clip(o_tiles[0][:, 0, :])
-        nc.sync.dma_start(out=out_view(0)[:, 0, :], in_=o_tiles[0][:, 0, :])
-        clip(o_tiles[0][:, 1, :])
-        nc.sync.dma_start(out=out_view(0)[:, 1, :], in_=o_tiles[0][:, 1, :])
-        quantise(6)
-        mx(2)
-        mx(3)
-        affine(2, "A")
-        affine(3, "A")
-        clip(o_tiles[1][:])
-        nc.sync.dma_start(out=out_view(1), in_=o_tiles[1][:])
-        quantise(7)
-        copy_out(11, "A")
-        transposes(12)
-        transposes(13)
-        mx(4)
-        mx(5)
-        affine(4, "A")
-        affine(5, "V")
-        clip(o_tiles[2][:])
-        nc.sync.dma_start(out=out_view(2), in_=o_tiles[2][:])
-        quantise(8)
-        mx(6)
-        mx(7)
-        affine(6, "A")
-        affine(7, "A")
-        clip(o_tiles[3][:])
-        nc.sync.dma_start(out=out_view(3), in_=o_tiles[3][:])
-        quantise(9)
-        copy_out(12, "A")
-        mx(8)
-        mx(9)
-        affine(8, "A")
-        affine(9, "V")
-        clip(o_tiles[4][:])
-        nc.sync.dma_start(out=out_view(4), in_=o_tiles[4][:])
-        quantise(10)
-        copy_out(13, "A")
-        transposes(14)
-        transposes(15)
-        mx(10)
-        mx(11)
-        affine(10, "A")
-        affine(11, "A")
-        clip(o_tiles[5][:])
-        nc.sync.dma_start(out=out_view(5), in_=o_tiles[5][:])
-        quantise(11)
-        mx(12)
-        mx(13)
-        affine(12, "A")
-        affine(13, "V")
-        clip(o_tiles[6][:])
-        nc.sync.dma_start(out=out_view(6), in_=o_tiles[6][:])
-        quantise(12)
-        copy_out(14, "A")
-        mx(14)
-        mx(15)
-        affine(14, "A")
-        affine(15, "A")
-        clip(o_tiles[7][:])
-        nc.sync.dma_start(out=out_view(7), in_=o_tiles[7][:])
-        quantise(13)
-        copy_out(15, "A")
-        mx(16)
-        mx(17)
-        affine(16, "A")
-        affine(17, "V")
-        clip(o_tiles[8][:])
-        nc.sync.dma_start(out=out_view(8), in_=o_tiles[8][:])
-        quantise(14)
-        mx(18)
-        mx(19)
-        affine(18, "A")
-        affine(19, "A")
-        clip(o_tiles[9][:])
-        nc.sync.dma_start(out=out_view(9), in_=o_tiles[9][:])
-        quantise(15)
-        mx(20)
-        mx(21)
-        affine(20, "A")
-        affine(21, "V")
-        clip(o_tiles[10][:])
-        nc.sync.dma_start(out=out_view(10), in_=o_tiles[10][:])
-        mx(22)
-        mx(23)
-        affine(22, "A")
-        affine(23, "A")
-        clip(o_tiles[11][:])
-        nc.sync.dma_start(out=out_view(11), in_=o_tiles[11][:])
-        mx(24)
-        mx(25)
-        affine(24, "A")
-        affine(25, "V")
-        clip(o_tiles[12][:])
-        nc.sync.dma_start(out=out_view(12), in_=o_tiles[12][:])
-        mx(26)
-        mx(27)
-        affine(26, "A")
-        affine(27, "A")
-        clip(o_tiles[13][:])
-        nc.sync.dma_start(out=out_view(13), in_=o_tiles[13][:])
-        mx(28)
-        mx(29)
-        affine(28, "A")
-        affine(29, "V")
-        clip(o_tiles[14][:])
-        nc.sync.dma_start(out=out_view(14), in_=o_tiles[14][:])
-        mx(30)
-        mx(31)
-        affine(30, "A")
-        affine(31, "V")
-        clip(o_tiles[15][:, 0, :])
-        nc.sync.dma_start(out=out_view(15)[:, 0, :], in_=o_tiles[15][:, 0, :])
-        clip(o_tiles[15][:, 1, :])
-        nc.sync.dma_start(out=out_view(15)[:, 1, :], in_=o_tiles[15][:, 1, :])
+        affine(0, "V")
+        affine(1, "A")
+        for j in range(2):
+            clip(o_tiles[0][:, j, :])
+            nc.sync.dma_start(out=out_view(0)[:, j, :], in_=o_tiles[0][:, j, :])
+        for c in range(1, NCH):
+            mx(2 * c)
+            mx(2 * c + 1)
+            affine(2 * c, "A")
+            affine(2 * c + 1, "V" if c % 2 == 1 else "A")
+            clip(o_tiles[c][:])
+            nc.sync.dma_start(out=out_view(c), in_=o_tiles[c][:])
+            if c in (2, 4):
+                copy_out(14 + (c - 2) // 2, "A")
+            if c in (1, 3, 5):
+                quantise(13 + (c - 1) // 2)

@@ -266,8 +266,8 @@ def tile_similaritymatrixlayer_kernel(tc, inputs, w, b, out):
 
         mx(0)
         mx(1)
-        affine(0, "V")
-        affine(1, "A")
+        affine(0, "A")
+        affine(1, "V")
         for j in range(2):
             clip(o_tiles[0][:, j, :])
             nc.sync.dma_start(out=out_view(0)[:, j, :], in_=o_tiles[0][:, j, :])
@@ -275,9 +275,17 @@ def tile_similaritymatrixlayer_kernel(tc, inputs, w, b, out):
             mx(2 * c)
             mx(2 * c + 1)
             affine(2 * c, "A")
-            affine(2 * c + 1, "V" if c % 2 == 1 else "A")
-            clip(o_tiles[c][:])
-            nc.sync.dma_start(out=out_view(c), in_=o_tiles[c][:])
+            if c % 2 == 1:
+                affine(2 * c + 1, "V")
+                for j in range(2):
+                    clip(o_tiles[c][:, j, :])
+                    if c == NCH - 1:
+                        nc.sync.dma_start(out=out_view(c)[:, j, :], in_=o_tiles[c][:, j, :])
+            else:
+                affine(2 * c + 1, "A")
+                clip(o_tiles[c][:])
+            if c < NCH - 1:
+                nc.sync.dma_start(out=out_view(c), in_=o_tiles[c][:])
             if c in (2, 4):
                 copy_out(14 + (c - 2) // 2, "A")
             if c in (1, 3, 5):

@@ -1,4 +1,3 @@
-import math
 from contextlib import ExitStack
 
 import concourse.mybir as mybir
@@ -44,6 +43,25 @@ def tile_similaritymatrixlayer_kernel(tc, inputs, w, b, out):
                         out=xu[:, 2 * K * h : 2 * K * (h + 1)],
                         in_=rows[256 * h : 256 * (h + 1), :].rearrange("(p j) k -> p (j k)", j=2),
                     )
+        wsrc = const.tile([P, 4 * SPK], BF16, name="wsrc", align_bytes=64)
+        nc.vector.memset(wsrc[:], 1.0)
+        wq = const.tile([P, SPK], U32, name="wq", align_bytes=64)
+        wsc = const.tile([P, SPK], U8, name="wsc", align_bytes=64)
+        nc.vector.quantize_mx(out=wq[:].bitcast(FP8X4), scales=wsc[:], in_=wsrc[:])
+
+        def idle_passes(n):
+            dm = psum.tile([P, SPK], F32, tag="wk", name="dm")
+            for i in range(n):
+                nc.tensor.matmul_mx(
+                    out=dm[:],
+                    lhsT=wq[:, 0:P].bitcast(FP8X4),
+                    lhsT_scale=wsc[:, 0:P],
+                    rhs=wq[:].bitcast(FP8X4),
+                    rhs_scale=wsc[:],
+                    start=True,
+                    stop=True,
+                )
+
         wb16 = const.tile([P, 32], BF16, name="wb16")
         nc.vector.memset(wb16[:], 0.0)
         nc.scalar.dma_start(out=wb16[0:1, 0:1], in_=w.rearrange("(o n) -> o n", o=1))
@@ -51,7 +69,7 @@ def tile_similaritymatrixlayer_kernel(tc, inputs, w, b, out):
 
         warm = const.tile([P, 1], F32, name="warm")
         nc.vector.memset(warm[:], 1.0)
-        nc.scalar.activation(out=warm[:], in_=warm[:], func=ACT.Sqrt)
+        nc.scalar.activation(out=warm[:], in_=warm[:], func=ACT.Abs_reciprocal_sqrt)
         ident = const.tile([P, P], F32, name="ident")
         make_identity(nc, ident[:])
         avg = {}
@@ -100,6 +118,8 @@ def tile_similaritymatrixlayer_kernel(tc, inputs, w, b, out):
             else:
                 bank, c0, wd, tiles = 1 + h, 32 * (u // 2), 32, (2 * h, 2 * h + 1)
             for t in range(4):
+                if t == 2 and u % 2 == 0:
+                    idle_passes(1)
                 for n, a in enumerate(tiles):
                     nc.tensor.matmul(
                         out=cm[bank][:, t, c0 : c0 + wd],
@@ -170,12 +190,11 @@ def tile_similaritymatrixlayer_kernel(tc, inputs, w, b, out):
             else:
                 nc.tensor.matmul(out=tot_ps[0][:], lhsT=ones[:], rhs=ss[:, NSS - 1 : NSS], start=False, stop=True)
 
-        def root():
-            nc.scalar.activation(out=norm[:], in_=tot_ps[0][:], func=ACT.Sqrt)
+        def floor_total():
+            nc.vector.tensor_scalar(out=norm[:], in0=tot_ps[0][:], scalar1=EPS, scalar2=None, op0=ALU.max)
 
-        def inverse():
-            nc.vector.tensor_scalar(out=norm[:], in0=norm[:], scalar1=math.sqrt(EPS), scalar2=None, op0=ALU.max)
-            nc.vector.reciprocal(out=rnorm[:], in_=norm[:])
+        def inverse_root():
+            nc.scalar.activation(out=rnorm[:], in_=norm[:], func=ACT.Abs_reciprocal_sqrt)
 
         def scale_bank(bk, eng):
             if bk in (0, 3):
@@ -230,10 +249,13 @@ def tile_similaritymatrixlayer_kernel(tc, inputs, w, b, out):
             r0 = 512 * u + 256 * h2
             return out[r0 : r0 + 256, :].rearrange("(p j) n -> p j n", j=2)
 
+        idle_passes(4)
         for u in range(NU):
             means(u, 0)
             if u == 7:
                 partial_total()
+            if u in (1, 3, 5):
+                idle_passes(1)
             if u % 2 == 1:
                 means(u, 1)
             if u == 2:
@@ -251,10 +273,10 @@ def tile_similaritymatrixlayer_kernel(tc, inputs, w, b, out):
         total(1)
         transposes(13)
         transposes(14)
-        root()
-        transposes(15)
         quantise(11)
-        inverse()
+        floor_total()
+        inverse_root()
+        transposes(15)
         scale_bank(0, "V")
         scale_bank(1, "A")
         scale_bank(3, "V")

@@ -43,14 +43,22 @@ def tile_similaritymatrixlayer_kernel(tc, inputs, w, b, out):
                         out=xu[:, 2 * K * h : 2 * K * (h + 1)],
                         in_=rows[256 * h : 256 * (h + 1), :].rearrange("(p j) k -> p (j k)", j=2),
                     )
-        wsrc = const.tile([P, 4 * SPK], BF16, name="wsrc", align_bytes=64)
-        nc.vector.memset(wsrc[:], 1.0)
-        wq = const.tile([P, SPK], U32, name="wq", align_bytes=64)
-        wsc = const.tile([P, SPK], U8, name="wsc", align_bytes=64)
+        wb16 = const.tile([P, 32], BF16, name="wb16")
+        nc.vector.memset(wb16[:], 0.0)
+        nc.scalar.dma_start(out=wb16[0:1, 0:1], in_=w.rearrange("(o n) -> o n", o=1))
+        nc.scalar.dma_start(out=wb16[0:1, 16:17], in_=b.rearrange("(o n) -> o n", o=1))
+        warm = const.tile([P, 1], F32, name="warm")
+        nc.vector.memset(warm[:], 1.0)
+        nc.scalar.activation(out=warm[:], in_=warm[:], func=ACT.Abs_reciprocal_sqrt)
+        NID = 256
+        wsrc = const.tile([P, 4 * NID], BF16, name="wsrc", align_bytes=64)
+        nc.vector.memset(wsrc[:].bitcast(F32), 1.0)
+        wq = const.tile([P, NID], U32, name="wq", align_bytes=64)
+        wsc = const.tile([P, NID], U8, name="wsc", align_bytes=64)
         nc.vector.quantize_mx(out=wq[:].bitcast(FP8X4), scales=wsc[:], in_=wsrc[:])
 
         def idle_passes(n):
-            dm = psum.tile([P, SPK], F32, tag="wk", name="dm")
+            dm = psum.tile([P, NID], F32, tag="wk", name="dm")
             for i in range(n):
                 nc.tensor.matmul_mx(
                     out=dm[:],
@@ -62,14 +70,7 @@ def tile_similaritymatrixlayer_kernel(tc, inputs, w, b, out):
                     stop=True,
                 )
 
-        wb16 = const.tile([P, 32], BF16, name="wb16")
-        nc.vector.memset(wb16[:], 0.0)
-        nc.scalar.dma_start(out=wb16[0:1, 0:1], in_=w.rearrange("(o n) -> o n", o=1))
-        nc.scalar.dma_start(out=wb16[0:1, 16:17], in_=b.rearrange("(o n) -> o n", o=1))
 
-        warm = const.tile([P, 1], F32, name="warm")
-        nc.vector.memset(warm[:], 1.0)
-        nc.scalar.activation(out=warm[:], in_=warm[:], func=ACT.Abs_reciprocal_sqrt)
         ident = const.tile([P, P], F32, name="ident")
         make_identity(nc, ident[:])
         avg = {}
@@ -118,8 +119,6 @@ def tile_similaritymatrixlayer_kernel(tc, inputs, w, b, out):
             else:
                 bank, c0, wd, tiles = 1 + h, 32 * (u // 2), 32, (2 * h, 2 * h + 1)
             for t in range(4):
-                if t == 2 and u % 2 == 0:
-                    idle_passes(1)
                 for n, a in enumerate(tiles):
                     nc.tensor.matmul(
                         out=cm[bank][:, t, c0 : c0 + wd],
@@ -249,13 +248,13 @@ def tile_similaritymatrixlayer_kernel(tc, inputs, w, b, out):
             r0 = 512 * u + 256 * h2
             return out[r0 : r0 + 256, :].rearrange("(p j) n -> p j n", j=2)
 
-        idle_passes(4)
+        idle_passes(8)
         for u in range(NU):
             means(u, 0)
             if u == 7:
                 partial_total()
             if u in (1, 3, 5):
-                idle_passes(1)
+                idle_passes(2)
             if u % 2 == 1:
                 means(u, 1)
             if u == 2:

@@ -183,9 +183,7 @@ def tile_similaritymatrixlayer_kernel(tc, inputs, w, b, out):
 
         def total(step):
             if step == 0:
-                tp = psum.tile([P, 1], F32, tag="wk", name="tot_ps")
-                tot_ps[0] = tp
-                nc.tensor.matmul(out=tp[:], lhsT=ones[:], rhs=part[:], start=True, stop=False)
+                nc.tensor.matmul(out=tot_ps[0][:], lhsT=ones[:], rhs=part[:], start=True, stop=False)
             else:
                 nc.tensor.matmul(out=tot_ps[0][:], lhsT=ones[:], rhs=ss[:, NSS - 1 : NSS], start=False, stop=True)
 
@@ -267,6 +265,8 @@ def tile_similaritymatrixlayer_kernel(tc, inputs, w, b, out):
                     copy_out(c, "V" if c % 4 == 3 else "A")
                     if c >= 1:
                         quantise(c - 1)
+        tp = psum.tile([P, 1], F32, tag="wk", name="tot_ps")
+        tot_ps[0] = tp
         transposes(12)
         total(0)
         total(1)
@@ -275,6 +275,7 @@ def tile_similaritymatrixlayer_kernel(tc, inputs, w, b, out):
         quantise(11)
         floor_total()
         inverse_root()
+        idle_passes(8)
         transposes(15)
         scale_bank(0, "V")
         scale_bank(1, "A")
@@ -285,29 +286,49 @@ def tile_similaritymatrixlayer_kernel(tc, inputs, w, b, out):
         copy_out(13, "A")
         quantise(12)
 
-        mx(0)
+        o0 = data.tile([P, 2, SPK], F32, name="o0")
+        o_tiles[0] = o0
+        half = {}
+        for g in range(2):
+            hg = psum.tile([P, SPK // 2], F32, tag="cm", name="half%d" % g)
+            half[g] = hg
+            nc.tensor.matmul_mx(
+                out=hg[:],
+                lhsT=xq[0][:, 0:P].bitcast(FP8X4),
+                lhsT_scale=xs[0][:, 0:P],
+                rhs=cq[:, 256 * g : 256 * (g + 1)].bitcast(FP8X4),
+                rhs_scale=cs[:, 256 * g : 256 * (g + 1)],
+                start=True,
+                stop=True,
+            )
         mx(1)
-        affine(0, "A")
-        affine(1, "V")
-        for j in range(2):
-            clip(o_tiles[0][:, j, :])
-            nc.sync.dma_start(out=out_view(0)[:, j, :], in_=o_tiles[0][:, j, :])
+        nc.scalar.activation(out=o0[:, 0, 0:256], in_=half[0][:], func=ACT.Relu, scale=absw[:, 0:1], bias=bias)
+        nc.vector.tensor_scalar(
+            out=o0[:, 0, 256:512], in0=half[1][:], scalar1=absw[:, 0:1], scalar2=bias, op0=ALU.mult, op1=ALU.add
+        )
+        affine(1, "A")
+        clip(o0[:, 0, 0:256])
+        clip(o0[:, 0, 256:512])
+        nc.sync.dma_start(out=out_view(0)[:, 0, :], in_=o0[:, 0, :])
+        clip(o0[:, 1, :])
+        nc.sync.dma_start(out=out_view(0)[:, 1, :], in_=o0[:, 1, :])
+        NFINE = 3
         for c in range(1, NCH):
+            fine = c <= NFINE or c == NCH - 1
             mx(2 * c)
             mx(2 * c + 1)
             affine(2 * c, "A")
-            if c % 2 == 1:
-                affine(2 * c + 1, "V")
+            affine(2 * c + 1, "V" if c % 2 == 1 else "A")
+            if c % 2 == 1 or fine:
                 for j in range(2):
                     clip(o_tiles[c][:, j, :])
-                    if c == NCH - 1:
+                    if fine:
                         nc.sync.dma_start(out=out_view(c)[:, j, :], in_=o_tiles[c][:, j, :])
             else:
-                affine(2 * c + 1, "A")
                 clip(o_tiles[c][:])
-            if c < NCH - 1:
+            if not fine:
                 nc.sync.dma_start(out=out_view(c), in_=o_tiles[c][:])
-            if c in (2, 4):
-                copy_out(14 + (c - 2) // 2, "A")
-            if c in (1, 3, 5):
-                quantise(13 + (c - 1) // 2)
+            if c in (8, 10):
+                copy_out(14 + (c - 8) // 2, "A")
+            if c in (7, 9, 11):
+                quantise(13 + (c - 7) // 2)

@@ -19,6 +19,7 @@ SPK = 512
 EPS = 1e-6
 NU = 8
 NCH = 16
+ORDER = (1, 0, 2, 3, 4, 6, 5, 7)
 FLOPS = 2 * ROWS * K * SPK
 
 
@@ -30,10 +31,10 @@ def tile_similaritymatrixlayer_kernel(tc, inputs, w, b, out):
         psum = ctx.enter_context(tc.psum_pool(name="psum", bufs=4))
         ctx.enter_context(tc.manual_schedule())
 
-        x = []
-        for u in range(NU):
+        x = {}
+        for u in ORDER:
             xu = data.tile([P, 4 * K], BF16, name="x%d" % u)
-            x.append(xu)
+            x[u] = xu
             rows = inputs[512 * u : 512 * (u + 1), :]
             if u % 2 == 0:
                 nc.sync.dma_start(out=xu[:], in_=rows.rearrange("(p a) k -> p (a k)", a=4))
@@ -74,7 +75,7 @@ def tile_similaritymatrixlayer_kernel(tc, inputs, w, b, out):
         ident = const.tile([P, P], F32, name="ident")
         make_identity(nc, ident[:])
         avg = {}
-        for wd in (64, 32):
+        for wd in (32, 64):
             avg_f = const.tile([P, wd], F32, name="avg_f%d" % wd)
             nc.vector.tensor_reduce(
                 out=avg_f[:], in_=ident[:].rearrange("p (s i) -> p s i", s=wd), axis=AX.X, op=ALU.add
@@ -246,80 +247,85 @@ def tile_similaritymatrixlayer_kernel(tc, inputs, w, b, out):
             r0 = 512 * u + 256 * h2
             return out[r0 : r0 + 256, :].rearrange("(p j) n -> p j n", j=2)
 
-        idle_passes(8)
-        for u in range(NU):
+        CH = []
+        for u in ORDER:
+            CH.extend((2 * u, 2 * u + 1))
+        idle_passes(4)
+        for k, u in enumerate(ORDER):
             means(u, 0)
-            if u == 7:
+            if k == NU - 1:
                 partial_total()
-            if u in (1, 3, 5):
+            if u % 2 == 1 and k < NU - 1:
                 idle_passes(2)
             if u % 2 == 1:
                 means(u, 1)
-            if u == 2:
+            if k == 2:
                 spread()
-            if u == 3:
+            if k == 3:
                 scale_and_bias()
-            if 1 <= u <= 6:
-                for c in (2 * u - 2, 2 * u - 1):
-                    transposes(c)
-                    copy_out(c, "V" if c % 4 == 3 else "A")
-                    if c >= 1:
-                        quantise(c - 1)
+            if 1 <= k <= 6:
+                for n in (2 * k - 2, 2 * k - 1):
+                    transposes(CH[n])
+                    copy_out(CH[n], "V" if n % 4 == 3 else "A")
+                    if n >= 1:
+                        quantise(CH[n - 1])
         tp = psum.tile([P, 1], F32, tag="wk", name="tot_ps")
         tot_ps[0] = tp
-        transposes(12)
+        transposes(CH[12])
         total(0)
         total(1)
-        transposes(13)
-        transposes(14)
-        quantise(11)
+        transposes(CH[13])
+        transposes(CH[14])
+        quantise(CH[11])
         floor_total()
         inverse_root()
         idle_passes(8)
-        transposes(15)
+        transposes(CH[15])
         scale_bank(0, "V")
         scale_bank(1, "A")
         scale_bank(3, "V")
         scale_bank(2, "A")
         nc.vector.quantize_mx(out=cq[:].bitcast(FP8X4), scales=cs[:], in_=cent[:])
-        copy_out(12, "A")
-        copy_out(13, "A")
-        quantise(12)
+        copy_out(CH[12], "A")
+        copy_out(CH[13], "A")
+        quantise(CH[12])
 
-        o0 = data.tile([P, 2, SPK], F32, name="o0")
-        o_tiles[0] = o0
+        c = CH[0]
+        o0 = data.tile([P, 2, SPK], F32, name="o_first")
+        o_tiles[c] = o0
         half = {}
         for g in range(2):
             hg = psum.tile([P, SPK // 2], F32, tag="cm", name="half%d" % g)
             half[g] = hg
             nc.tensor.matmul_mx(
                 out=hg[:],
-                lhsT=xq[0][:, 0:P].bitcast(FP8X4),
-                lhsT_scale=xs[0][:, 0:P],
+                lhsT=xq[c][:, 0:P].bitcast(FP8X4),
+                lhsT_scale=xs[c][:, 0:P],
                 rhs=cq[:, 256 * g : 256 * (g + 1)].bitcast(FP8X4),
                 rhs_scale=cs[:, 256 * g : 256 * (g + 1)],
                 start=True,
                 stop=True,
             )
-        mx(1)
+        mx(2 * c + 1)
         nc.scalar.activation(out=o0[:, 0, 0:256], in_=half[0][:], func=ACT.Relu, scale=absw[:, 0:1], bias=bias)
         nc.vector.tensor_scalar(
             out=o0[:, 0, 256:512], in0=half[1][:], scalar1=absw[:, 0:1], scalar2=bias, op0=ALU.mult, op1=ALU.add
         )
-        affine(1, "A")
+        affine(2 * c + 1, "A")
         clip(o0[:, 0, 0:256])
         clip(o0[:, 0, 256:512])
-        nc.sync.dma_start(out=out_view(0)[:, 0, :], in_=o0[:, 0, :])
+        nc.sync.dma_start(out=out_view(c)[:, 0, :], in_=o0[:, 0, :])
         clip(o0[:, 1, :])
-        nc.sync.dma_start(out=out_view(0)[:, 1, :], in_=o0[:, 1, :])
+        nc.sync.dma_start(out=out_view(c)[:, 1, :], in_=o0[:, 1, :])
         NFINE = 3
-        for c in range(1, NCH):
-            fine = c <= NFINE or c == NCH - 1
+        for n in range(1, NCH):
+            c = CH[n]
+            fine = n <= NFINE or n == NCH - 1
             mx(2 * c)
             mx(2 * c + 1)
             affine(2 * c, "A")
-            affine(2 * c + 1, "V" if c % 2 == 1 else "A")
-            if c % 2 == 1 or fine:
+            affine(2 * c + 1, "V" if n % 2 == 1 else "A")
+            if n % 2 == 1 or fine:
                 for j in range(2):
                     clip(o_tiles[c][:, j, :])
                     if fine:
@@ -328,7 +334,7 @@ def tile_similaritymatrixlayer_kernel(tc, inputs, w, b, out):
                 clip(o_tiles[c][:])
             if not fine:
                 nc.sync.dma_start(out=out_view(c), in_=o_tiles[c][:])
-            if c in (8, 10):
-                copy_out(14 + (c - 8) // 2, "A")
-            if c in (7, 9, 11):
-                quantise(13 + (c - 7) // 2)
+            if n in (8, 10):
+                copy_out(CH[14 + (n - 8) // 2], "A")
+            if n in (7, 9, 11):
+                quantise(CH[13 + (n - 7) // 2])

@@ -255,8 +255,6 @@ def tile_similaritymatrixlayer_kernel(tc, inputs, w, b, out):
             means(u, 0)
             if k == NU - 1:
                 partial_total()
-            if u % 2 == 1 and k < NU - 1:
-                idle_passes(2)
             if u % 2 == 1:
                 means(u, 1)
             if k == 2:

@@ -263,20 +263,23 @@ def tile_similaritymatrixlayer_kernel(tc, inputs, w, b, out):
                 scale_and_bias()
             if 1 <= k <= 6:
                 for n in (2 * k - 2, 2 * k - 1):
-                    transposes(CH[n])
-                    copy_out(CH[n], "V" if n % 4 == 3 else "A")
-                    if n >= 1:
-                        quantise(CH[n - 1])
+                    if n < 11:
+                        transposes(CH[n])
+                        copy_out(CH[n], "V" if n % 4 == 3 else "A")
+                        if n >= 1:
+                            quantise(CH[n - 1])
         tp = psum.tile([P, 1], F32, tag="wk", name="tot_ps")
         tot_ps[0] = tp
-        transposes(CH[12])
+        transposes(CH[11])
         total(0)
         total(1)
+        quantise(CH[10])
+        copy_out(CH[11], "V")
+        transposes(CH[12])
         transposes(CH[13])
-        transposes(CH[14])
-        quantise(CH[11])
         floor_total()
         inverse_root()
+        transposes(CH[14])
         idle_passes(8)
         transposes(CH[15])
         scale_bank(0, "V")
@@ -286,6 +289,7 @@ def tile_similaritymatrixlayer_kernel(tc, inputs, w, b, out):
         nc.vector.quantize_mx(out=cq[:].bitcast(FP8X4), scales=cs[:], in_=cent[:])
         copy_out(CH[12], "A")
         copy_out(CH[13], "A")
+        quantise(CH[11])
         quantise(CH[12])
 
         c = CH[0]

@@ -256,6 +256,7 @@ def tile_similaritymatrixlayer_kernel(tc, inputs, w, b, out):
             if k == NU - 1:
                 partial_total()
             if u % 2 == 1:
+                idle_passes(2)
                 means(u, 1)
             if k == 2:
                 spread()
@@ -273,14 +274,15 @@ def tile_similaritymatrixlayer_kernel(tc, inputs, w, b, out):
         transposes(CH[11])
         total(0)
         total(1)
+        idle_passes(4)
         quantise(CH[10])
         copy_out(CH[11], "V")
         transposes(CH[12])
-        transposes(CH[13])
         floor_total()
         inverse_root()
+        transposes(CH[13])
         transposes(CH[14])
-        idle_passes(8)
+        idle_passes(4)
         transposes(CH[15])
         scale_bank(0, "V")
         scale_bank(1, "A")

from contextlib import ExitStack

import concourse.mybir as mybir
from concourse.masks import make_identity

F32 = mybir.dt.float32
BF16 = mybir.dt.bfloat16
U32 = mybir.dt.uint32
U8 = mybir.dt.uint8
FP8X4 = mybir.dt.float8_e4m3fn_x4
ALU = mybir.AluOpType
ACT = mybir.ActivationFunctionType
AX = mybir.AxisListType

P = 128
ROWS = 4096
K = 512
SPK = 512
EPS = 1e-6
NU = 8
NCH = 16
ORDER = (1, 0, 2, 3, 4, 6, 5, 7)
FLOPS = 2 * ROWS * K * SPK


def tile_similaritymatrixlayer_kernel(tc, inputs, w, b, out):
    nc = tc.nc
    with ExitStack() as ctx:
        const = ctx.enter_context(tc.tile_pool(name="const", bufs=1))
        data = ctx.enter_context(tc.tile_pool(name="data", bufs=1))
        psum = ctx.enter_context(tc.psum_pool(name="psum", bufs=4))
        ctx.enter_context(tc.manual_schedule())

        x = {}
        for u in ORDER:
            xu = data.tile([P, 4 * K], BF16, name="x%d" % u)
            x[u] = xu
            rows = inputs[512 * u : 512 * (u + 1), :]
            if u % 2 == 0:
                nc.sync.dma_start(out=xu[:], in_=rows.rearrange("(p a) k -> p (a k)", a=4))
            else:
                for h in range(2):
                    nc.sync.dma_start(
                        out=xu[:, 2 * K * h : 2 * K * (h + 1)],
                        in_=rows[256 * h : 256 * (h + 1), :].rearrange("(p j) k -> p (j k)", j=2),
                    )
        wb16 = const.tile([P, 32], BF16, name="wb16")
        nc.vector.memset(wb16[:], 0.0)
        nc.scalar.dma_start(out=wb16[0:1, 0:1], in_=w.rearrange("(o n) -> o n", o=1))
        nc.scalar.dma_start(out=wb16[0:1, 16:17], in_=b.rearrange("(o n) -> o n", o=1))
        warm = const.tile([P, 1], F32, name="warm")
        nc.vector.memset(warm[:], 1.0)
        nc.scalar.activation(out=warm[:], in_=warm[:], func=ACT.Abs_reciprocal_sqrt)
        NID = 256
        wsrc = const.tile([P, 4 * NID], BF16, name="wsrc", align_bytes=64)
        nc.vector.memset(wsrc[:].bitcast(F32), 1.0)
        wq = const.tile([P, NID], U32, name="wq", align_bytes=64)
        wsc = const.tile([P, NID], U8, name="wsc", align_bytes=64)
        nc.vector.quantize_mx(out=wq[:].bitcast(FP8X4), scales=wsc[:], in_=wsrc[:])

        def idle_passes(n):
            dm = psum.tile([P, NID], F32, tag="wk", name="dm")
            for i in range(n):
                nc.tensor.matmul_mx(
                    out=dm[:],
                    lhsT=wq[:, 0:P].bitcast(FP8X4),
                    lhsT_scale=wsc[:, 0:P],
                    rhs=wq[:].bitcast(FP8X4),
                    rhs_scale=wsc[:],
                    start=True,
                    stop=True,
                )


        ident = const.tile([P, P], F32, name="ident")
        make_identity(nc, ident[:])
        avg = {}
        for wd in (32, 64):
            avg_f = const.tile([P, wd], F32, name="avg_f%d" % wd)
            nc.vector.tensor_reduce(
                out=avg_f[:], in_=ident[:].rearrange("p (s i) -> p s i", s=wd), axis=AX.X, op=ALU.add
            )
            avg_b = const.tile([P, wd], BF16, name="avg_b%d" % wd)
            nc.vector.tensor_scalar(out=avg_b[:], in0=avg_f[:], scalar1=0.125, scalar2=None, op0=ALU.mult)
            avg[wd] = avg_b
        ones = const.tile([P, P], F32, name="ones")
        nc.vector.memset(ones[:], 1.0)

        ones16 = const.tile([P, P], BF16, name="ones16")
        nc.vector.memset(ones16[:], 1.0)
        wbf = const.tile([P, 32], F32, name="wbf")
        negw = const.tile([P, 1], F32, name="negw")
        absw = const.tile([P, 1], F32, name="absw")
        bias = wbf[:, 16:17]
        wb_ps = {}

        def spread():
            wp = psum.tile([P, 32], F32, tag="wk", name="wb_ps")
            wb_ps[0] = wp
            nc.tensor.matmul(out=wp[:], lhsT=ones16[:], rhs=wb16[:], start=True, stop=True)

        def scale_and_bias():
            nc.vector.tensor_copy(out=wbf[:], in_=wb_ps[0][:])
            nc.vector.tensor_scalar(out=negw[:], in0=wbf[:, 0:1], scalar1=-1.0, scalar2=None, op0=ALU.mult)
            nc.vector.tensor_tensor(out=absw[:], in0=wbf[:, 0:1], in1=negw[:], op=ALU.max)

        cm = []
        for bk in range(4):
            cmb = psum.tile([P, 4, P], F32, tag="cm", name="cm%d" % bk)
            cm.append(cmb)
        NSS = 12
        ss = const.tile([P, NSS], F32, name="ss")
        junk = const.tile([P, 4, 64], F32, name="junk")
        ss_col = [0]

        def means(u, h):
            xv = x[u][:].rearrange("p (a u q e) -> p a u e q", a=4, u=2, q=P, e=2)
            if u % 2 == 0:
                bank, c0, wd, tiles = (0 if u % 4 == 0 else 3), 64 * (u // 4), 64, (0, 1, 2, 3)
            else:
                bank, c0, wd, tiles = 1 + h, 32 * (u // 2), 32, (2 * h, 2 * h + 1)
            for t in range(4):
                for n, a in enumerate(tiles):
                    nc.tensor.matmul(
                        out=cm[bank][:, t, c0 : c0 + wd],
                        lhsT=xv[:, a, t // 2, t % 2, :],
                        rhs=avg[wd][:],
                        start=(n == 0),
                        stop=(n == len(tiles) - 1),
                    )
            col = ss_col[0]
            ss_col[0] = col + 1
            nc.scalar.activation(
                out=junk[:, :, 0:wd],
                in_=cm[bank][:, :, c0 : c0 + wd],
                func=ACT.Square,
                accum_out=ss[:, col : col + 1],
            )

        grp = {}
        xq = {}
        xs = {}
        xts = {}

        def transposes(c):
            xw = x[c // 2][:].bitcast(F32)
            xt = psum.tile([P, 2, 2, P], F32, tag="wk", name="xt")
            xts[c] = xt
            for jj in range(2):
                for u2 in range(2):
                    c0 = 256 * (2 * (c % 2) + jj) + P * u2
                    nc.tensor.transpose(xt[:, jj, u2, :], xw[:, c0 : c0 + P], ident[:])

        def copy_out(c, eng):
            gc = data.tile([P, 2 * P * 4], BF16, name="g%d" % c, align_bytes=64)
            grp[c] = gc
            dst = grp[c][:].bitcast(F32).rearrange("q (j r u) -> q j r u", j=2, r=P, u=2)
            srcx = xts[c][:].rearrange("q j u r -> q j r u")
            if eng == "V":
                nc.vector.tensor_copy(out=dst, in_=srcx)
            else:
                nc.scalar.copy(out=dst, in_=srcx)

        def quantise(c):
            xqc = data.tile([P, 2 * P], U32, name="xq%d" % c, align_bytes=64)
            xq[c] = xqc
            xsc = data.tile([P, 2 * P], U8, name="xs%d" % c, align_bytes=64)
            xs[c] = xsc
            nc.vector.quantize_mx(out=xq[c][:].bitcast(FP8X4), scales=xs[c][:], in_=grp[c][:])

        norm = const.tile([P, 1], F32, name="norm")
        rnorm = const.tile([P, 1], F32, name="rnorm")
        cent = data.tile([P, SPK * 4], BF16, name="cent", align_bytes=64)
        cq = data.tile([P, SPK], U32, name="cq", align_bytes=64)
        cs = data.tile([P, SPK], U8, name="cs", align_bytes=64)
        cent64 = cent[:].rearrange("q (g r i t) -> q r g i t", g=2, r=4, i=64, t=4)
        cent32 = cent[:].rearrange("q (v r i t) -> q r v i t", v=4, r=4, i=32, t=4)
        tot_ps = {}

        part = const.tile([P, 1], F32, name="part")

        def partial_total():
            nc.vector.tensor_reduce(out=part[:], in_=ss[:, 0 : NSS - 1], axis=AX.X, op=ALU.add)

        def total(step):
            if step == 0:
                nc.tensor.matmul(out=tot_ps[0][:], lhsT=ones[:], rhs=part[:], start=True, stop=False)
            else:
                nc.tensor.matmul(out=tot_ps[0][:], lhsT=ones[:], rhs=ss[:, NSS - 1 : NSS], start=False, stop=True)

        def floor_total():
            nc.vector.tensor_scalar(out=norm[:], in0=tot_ps[0][:], scalar1=EPS, scalar2=None, op0=ALU.max)

        def inverse_root():
            nc.scalar.activation(out=rnorm[:], in_=norm[:], func=ACT.Abs_reciprocal_sqrt)

        def scale_bank(bk, eng):
            if bk in (0, 3):
                dst = cent64[:, 0 if bk == 0 else 2]
                srcc = cm[bk][:].rearrange("q t (g i) -> q g i t", g=2)
            else:
                dst = cent32[:, 1 + bk]
                srcc = cm[bk][:].rearrange("q t (v i) -> q v i t", v=4)
            if eng == "V":
                nc.vector.tensor_scalar(out=dst, in0=srcc, scalar1=rnorm[:, 0:1], scalar2=None, op0=ALU.mult)
            else:
                nc.scalar.activation(out=dst, in_=srcc, func=ACT.Copy, scale=rnorm[:, 0:1])

        o_tiles = {}
        accs = {}

        def mx(i):
            c, j = i // 2, i % 2
            acc = psum.tile([P, SPK], F32, tag="cm", name="acc")
            accs[i] = acc
            nc.tensor.matmul_mx(
                out=acc[:],
                lhsT=xq[c][:, P * j : P * (j + 1)].bitcast(FP8X4),
                lhsT_scale=xs[c][:, P * j : P * (j + 1)],
                rhs=cq[:].bitcast(FP8X4),
                rhs_scale=cs[:],
                start=True,
                stop=True,
            )

        def affine(i, eng):
            if i % 2 == 0:
                oc = data.tile([P, 2, SPK], F32, name="o%d" % (i // 2))
                o_tiles[i // 2] = oc
            dst = o_tiles[i // 2][:, i % 2, :]
            if eng == "V":
                nc.vector.tensor_scalar(
                    out=dst, in0=accs[i][:], scalar1=absw[:, 0:1], scalar2=bias, op0=ALU.mult, op1=ALU.add
                )
            else:
                nc.scalar.activation(
                    out=dst, in_=accs[i][:], func=ACT.Relu, scale=absw[:, 0:1], bias=bias
                )

        def clip(ap):
            nc.vector.tensor_scalar(out=ap, in0=ap, scalar1=0.0, scalar2=1.0, op0=ALU.max, op1=ALU.min)

        def out_view(c):
            u, h2 = c // 2, c % 2
            if u % 2 == 0:
                return out[512 * u : 512 * (u + 1), :].rearrange("(p a) n -> p a n", a=4)[:, 2 * h2 : 2 * h2 + 2, :]
            r0 = 512 * u + 256 * h2
            return out[r0 : r0 + 256, :].rearrange("(p j) n -> p j n", j=2)

        CH = []
        for u in ORDER:
            CH.extend((2 * u, 2 * u + 1))
        idle_passes(4)
        for k, u in enumerate(ORDER):
            means(u, 0)
            if k == NU - 1:
                partial_total()
            if u % 2 == 1:
                idle_passes(2)
                means(u, 1)
            if k == 2:
                spread()
            if k == 3:
                scale_and_bias()
            if 1 <= k <= 6:
                for n in (2 * k - 2, 2 * k - 1):
                    if n < 11:
                        transposes(CH[n])
                        copy_out(CH[n], "V" if n % 4 == 3 else "A")
                        if n >= 1:
                            quantise(CH[n - 1])
        tp = psum.tile([P, 1], F32, tag="wk", name="tot_ps")
        tot_ps[0] = tp
        transposes(CH[11])
        total(0)
        total(1)
        idle_passes(4)
        quantise(CH[10])
        copy_out(CH[11], "V")
        transposes(CH[12])
        floor_total()
        inverse_root()
        transposes(CH[13])
        transposes(CH[14])
        idle_passes(4)
        transposes(CH[15])
        scale_bank(0, "V")
        scale_bank(1, "A")
        scale_bank(3, "V")
        scale_bank(2, "A")
        nc.vector.quantize_mx(out=cq[:].bitcast(FP8X4), scales=cs[:], in_=cent[:])
        copy_out(CH[12], "A")
        copy_out(CH[13], "A")
        quantise(CH[11])
        quantise(CH[12])

        c = CH[0]
        o0 = data.tile([P, 2, SPK], F32, name="o_first")
        o_tiles[c] = o0
        half = {}
        for g in range(2):
            hg = psum.tile([P, SPK // 2], F32, tag="cm", name="half%d" % g)
            half[g] = hg
            nc.tensor.matmul_mx(
                out=hg[:],
                lhsT=xq[c][:, 0:P].bitcast(FP8X4),
                lhsT_scale=xs[c][:, 0:P],
                rhs=cq[:, 256 * g : 256 * (g + 1)].bitcast(FP8X4),
                rhs_scale=cs[:, 256 * g : 256 * (g + 1)],
                start=True,
                stop=True,
            )
        mx(2 * c + 1)
        nc.scalar.activation(out=o0[:, 0, 0:256], in_=half[0][:], func=ACT.Relu, scale=absw[:, 0:1], bias=bias)
        nc.vector.tensor_scalar(
            out=o0[:, 0, 256:512], in0=half[1][:], scalar1=absw[:, 0:1], scalar2=bias, op0=ALU.mult, op1=ALU.add
        )
        affine(2 * c + 1, "A")
        clip(o0[:, 0, 0:256])
        clip(o0[:, 0, 256:512])
        nc.sync.dma_start(out=out_view(c)[:, 0, :], in_=o0[:, 0, :])
        clip(o0[:, 1, :])
        nc.sync.dma_start(out=out_view(c)[:, 1, :], in_=o0[:, 1, :])
        NFINE = 3
        for n in range(1, NCH):
            c = CH[n]
            fine = n <= NFINE or n == NCH - 1
            mx(2 * c)
            mx(2 * c + 1)
            affine(2 * c, "A")
            affine(2 * c + 1, "V" if n % 2 == 1 else "A")
            if n % 2 == 1 or fine:
                for j in range(2):
                    clip(o_tiles[c][:, j, :])
                    if fine:
                        nc.sync.dma_start(out=out_view(c)[:, j, :], in_=o_tiles[c][:, j, :])
            else:
                clip(o_tiles[c][:])
            if not fine:
                nc.sync.dma_start(out=out_view(c), in_=o_tiles[c][:])
            if n in (8, 10):
                copy_out(CH[14 + (n - 8) // 2], "A")
            if n in (7, 9, 11):
                quantise(CH[13 + (n - 7) // 2])
